import numpy as np
import ml_dtypes

BF16 = ml_dtypes.bfloat16


def bf(x):
    return np.asarray(x, np.float32).astype(BF16)


def f32(x):
    return np.asarray(x, np.float32)


def f64(x):
    return np.asarray(x).astype(np.float64)


def striped(idx):
    return np.tile(idx.reshape(-1, 16).T, (8, 1))


D, S, N, GH, GW, WIN = 512, 4096, 1024, 32, 32, 9
EPS = 1e-5


def local_causal():
    t = np.arange(N)
    r, c = t // GW, t % GW
    return (np.abs(r[:, None] - r[None, :]) <= WIN) & (np.abs(c[:, None] - c[None, :]) <= WIN) & (t[:, None] <= t[None, :])


def setup_inputs():
    table = f32(np.random.standard_normal((D, S)))
    row = 0.5 * np.random.standard_normal((D // 2, GH))
    col = 0.5 * np.random.standard_normal((D // 2, GW))
    pos = f32(np.concatenate([np.repeat(row, GW, axis=1), np.tile(col, (1, GH))], axis=0))
    wq = bf(np.random.standard_normal((D, D)) / np.sqrt(D))
    wk = bf(np.random.standard_normal((D, D)) / np.sqrt(D))
    wv = bf(np.random.standard_normal((D, D)) / np.sqrt(D))
    bv = f32(0.1 * np.random.standard_normal((D, 1)))
    wo = bf(np.random.standard_normal((D, D)) / np.sqrt(D))
    bo = f32(0.1 * np.random.standard_normal((D, 1)))
    ln_gain = f32(1.0 + 0.1 * np.random.standard_normal((D, 1)))
    ln_bias = f32(0.1 * np.random.standard_normal((D, 1)))
    allow = f32(local_causal())
    idx = np.random.permutation(np.tile(np.arange(S), 2))[:N]
    return {"table": table, "pos": pos, "wq": wq, "wk": wk, "wv": wv, "bv": bv, "wo": wo, "bo": bo, "ln_gain": ln_gain, "ln_bias": ln_bias, "allow": allow, "offs": striped(idx)}


def reference(table, pos, wq, wk, wv, bv, wo, bo, ln_gain, ln_bias, allow, offs):
    idx = offs[:16].T.reshape(-1)
    h = f64(table)[:, idx] + f64(pos)
    q = f64(wq).T @ h
    k = f64(wk).T @ h
    v = f64(wv).T @ h + f64(bv)
    e = f64(allow) * np.exp((k.T @ q) / np.sqrt(D))
    a = e / e.sum(axis=0, keepdims=True)
    att = v @ a
    z = h + f64(wo).T @ att + f64(bo)
    mu = z.mean(axis=0, keepdims=True)
    var = ((z - mu) ** 2).mean(axis=0, keepdims=True)
    return (z - mu) / np.sqrt(var + EPS) * f64(ln_gain) + f64(ln_bias)

@@ -1,0 +1,271 @@
+import math
+
+import concourse.mybir as mybir
+from concourse.masks import make_identity
+
+F32, BF16, U16 = mybir.dt.float32, mybir.dt.bfloat16, mybir.dt.uint16
+ADD, SUB, MULT = mybir.AluOpType.add, mybir.AluOpType.subtract, mybir.AluOpType.mult
+FUNC = mybir.ActivationFunctionType
+ALONG_FREE = mybir.AxisListType.X
+
+P = 128
+D = 512
+WORDS = 4096
+N = 1024
+GRID = 32
+WIN = 9
+EPS = 1e-5
+
+CB = D // P
+NB = N // P
+HALF = 512
+REACH = WIN * GRID + WIN
+BACK = -(-REACH // P)
+SEEN = (BACK + 1) * P
+CHUNK = 2 * P
+SHUT = 1e30
+
+NEAR = sum(GRID - d for d in range(1, WIN + 1))
+PAIRS = NEAR * (GRID + 2 * NEAR) + GRID * (GRID + NEAR)
+FLOPS = 4 * 2 * D * D * N + 2 * 2 * D * PAIRS
+
+
+def tile_autoregressivemodel_b_kernel(
+    tc, table, pos, wq, wk, wv, bv, wo, bo, ln_gain, ln_bias, allow, offs, out
+):
+    nc = tc.nc
+    with (
+        tc.tile_pool(name="held", bufs=1) as held,
+        tc.psum_pool(name="psum_acc", bufs=3) as psum_acc,
+        tc.psum_pool(name="psum_score", bufs=2) as psum_score,
+        tc.psum_pool(name="psum_flip", bufs=1) as psum_flip,
+        tc.psum_pool(name="psum_stat", bufs=2) as psum_stat,
+    ):
+        offsets = held.tile([P, N // 16], U16, name="offsets")
+        nc.sync.dma_start(offsets[:], offs)
+
+        rows = held.tile([P, P], F32, name="rows")
+        nc.vector.memset(rows[:], 0.0)
+        for k, vec in enumerate((bo, ln_gain, ln_bias)):
+            nc.sync.dma_start(
+                rows[k * CB : (k + 1) * CB, :], vec.rearrange("(c p) o -> c (p o)", p=P)
+            )
+
+        weight_sb = {}
+        for name, w in (("wq", wq), ("wk", wk), ("wv", wv), ("wo", wo)):
+            weight_sb[name] = held.tile([P, CB, D], BF16, name=name + "_sb")
+        bv_all = held.tile([P, D], F32, name="bv_all")
+        allow_sb = [
+            held.tile([P, min(SEEN, N - kb * P)], F32, name=f"allow_sb{kb}") for kb in range(NB)
+        ]
+        h = [held.tile([P, N], F32, name=f"h{c}") for c in range(CB)]
+        h_bf = [held.tile([P, N], BF16, name=f"h_bf{c}") for c in range(CB)]
+
+        with tc.tile_pool(name="load", bufs=1) as load:
+            table_sb = [load.tile([P, WORDS], F32, name=f"table_sb{c}") for c in range(CB)]
+            pos_sb = [load.tile([P, N], F32, name=f"pos_sb{c}") for c in range(CB)]
+            for c in range(CB):
+                nc.sync.dma_start(table_sb[c][:], table[c * P : (c + 1) * P, :])
+                nc.sync.dma_start(pos_sb[c][:], pos[c * P : (c + 1) * P, :])
+            for name, w in (("wq", wq), ("wk", wk), ("wv", wv)):
+                nc.sync.dma_start(weight_sb[name][:], w.rearrange("(c p) d -> p c d", p=P))
+            nc.sync.dma_start(bv_all[:], bv.rearrange("d o -> (d o)").partition_broadcast(P))
+            for kb in range(NB):
+                width = min(SEEN, N - kb * P)
+                nc.sync.dma_start(
+                    allow_sb[kb][:], allow[kb * P : (kb + 1) * P, kb * P : kb * P + width]
+                )
+            nc.sync.dma_start(weight_sb["wo"][:], wo.rearrange("(c p) d -> p c d", p=P))
+
+            for c in range(CB):
+                nc.vector.tensor_tensor(
+                    h[c][:], table_sb[c][:].indirect(offsets[:]), pos_sb[c][:], ADD
+                )
+                nc.vector.tensor_copy(h_bf[c][:], h[c][:])
+
+        ident_f32 = held.tile([P, P], F32, name="ident_f32")
+        make_identity(nc, ident_f32[:])
+        ident_bf16 = held.tile([P, P], BF16, name="ident_bf16")
+        nc.vector.tensor_copy(ident_bf16[:], ident_f32[:])
+        mean_w = held.tile([P, P], BF16, name="mean_w")
+        nc.vector.memset(mean_w[:], 1.0 / D)
+        eps_col = held.tile([P, 1], F32, name="eps_col")
+        nc.vector.memset(eps_col[:], EPS)
+
+        cols_ps = psum_flip.tile([P, P], F32, tag="flip")
+        nc.tensor.transpose(cols_ps[:], rows[:], ident_f32[:])
+        cols = held.tile([P, 3 * CB], F32, name="cols")
+        nc.vector.tensor_copy(cols[:], cols_ps[:, : 3 * CB])
+        bo_col = [cols[:, m : m + 1] for m in range(CB)]
+        gain_col = [cols[:, CB + m : CB + m + 1] for m in range(CB)]
+        bias_col = [cols[:, 2 * CB + m : 2 * CB + m + 1] for m in range(CB)]
+
+        q_bf = [held.tile([P, N], BF16, name=f"q_bf{d}") for d in range(CB)]
+        k_bf = [held.tile([P, N], BF16, name=f"k_bf{d}") for d in range(CB)]
+        v_bf = [held.tile([P, D], BF16, name=f"v_bf{i}") for i in range(NB)]
+        for half in range(N // HALF):
+            span = slice(half * HALF, (half + 1) * HALF)
+            for d in range(CB):
+                q_ps = psum_acc.tile([P, HALF], F32, tag="acc")
+                for c in range(CB):
+                    nc.tensor.matmul(
+                        q_ps[:],
+                        weight_sb["wq"][:, c, d * P : (d + 1) * P],
+                        h_bf[c][:, span],
+                        start=(c == 0),
+                        stop=(c == CB - 1),
+                    )
+                nc.scalar.copy(q_bf[d][:, span], q_ps[:])
+                k_ps = psum_acc.tile([P, HALF], F32, tag="acc")
+                for c in range(CB):
+                    nc.tensor.matmul(
+                        k_ps[:],
+                        weight_sb["wk"][:, c, d * P : (d + 1) * P],
+                        h_bf[c][:, span],
+                        start=(c == 0),
+                        stop=(c == CB - 1),
+                    )
+                nc.scalar.copy(k_bf[d][:, span], k_ps[:])
+            for i in range(half * HALF // P, (half + 1) * HALF // P):
+                v_ps = psum_acc.tile([P, D], F32, tag="acc")
+                for c in range(CB):
+                    nc.tensor.matmul(
+                        v_ps[:],
+                        h_bf[c][:, i * P : (i + 1) * P],
+                        weight_sb["wv"][:, c, :],
+                        start=(c == 0),
+                        stop=(c == CB - 1),
+                    )
+                nc.vector.tensor_tensor(v_bf[i][:], v_ps[:], bv_all[:], ADD)
+
+        shut = [held.tile([P, SEEN], F32, name=f"shut{b}") for b in range(NB)]
+        for b in range(NB):
+            first = max(0, b - BACK)
+            seen = (b + 1 - first) * P
+            allow_flip = psum_score.tile([P, SEEN], F32, tag="score")
+            for kb in range(first, b + 1):
+                nc.tensor.transpose(
+                    allow_flip[:, (kb - first) * P : (kb - first + 1) * P],
+                    allow_sb[kb][:, (b - kb) * P : (b - kb + 1) * P],
+                    ident_f32[:],
+                )
+            nc.vector.tensor_scalar(shut[b][:, :seen], allow_flip[:, :seen], 1.0, SHUT, SUB, MULT)
+
+        weights = held.tile([P, NB, N], BF16, name="weights")
+
+        with (
+            tc.tile_pool(name="soft", bufs=2) as soft,
+            tc.tile_pool(name="tiny", bufs=4) as tiny,
+            tc.tile_pool(name="tail", bufs=2) as tail,
+            tc.tile_pool(name="store", bufs=4) as store,
+        ):
+            for b in range(NB):
+                first = max(0, b - BACK)
+                seen = (b + 1 - first) * P
+                score_ps = psum_score.tile([P, SEEN], F32, tag="score")
+                for d in range(CB):
+                    nc.tensor.matmul(
+                        score_ps[:, :seen],
+                        q_bf[d][:, b * P : (b + 1) * P],
+                        k_bf[d][:, first * P : (b + 1) * P],
+                        start=(d == 0),
+                        stop=(d == CB - 1),
+                    )
+                masked = soft.tile([P, SEEN], F32)
+                nc.vector.scalar_tensor_tensor(
+                    masked[:, :seen],
+                    score_ps[:, :seen],
+                    1.0 / math.sqrt(D),
+                    shut[b][:, :seen],
+                    MULT,
+                    ADD,
+                )
+                top = tiny.tile([P, 1], F32)
+                nc.vector.reduce_max(top[:], masked[:, :seen], axis=ALONG_FREE)
+                neg_top = tiny.tile([P, 1], F32)
+                nc.vector.tensor_scalar_mul(neg_top[:], top[:], -1.0)
+                e = soft.tile([P, SEEN], F32)
+                total = tiny.tile([P, 1], F32)
+                nc.scalar.activation(
+                    e[:, :seen], masked[:, :seen], FUNC.Exp, bias=neg_top[:], accum_out=total[:]
+                )
+                inv_total = tiny.tile([P, 1], F32)
+                nc.vector.reciprocal(inv_total[:], total[:])
+                a = soft.tile([P, SEEN], BF16)
+                nc.vector.tensor_scalar_mul(a[:, :seen], e[:, :seen], inv_total[:])
+                a_flip = psum_flip.tile([P, SEEN], BF16, tag="flip")
+                for kk in range(b + 1 - first):
+                    nc.tensor.transpose(
+                        a_flip[:, kk * P : (kk + 1) * P], a[:, kk * P : (kk + 1) * P], ident_bf16[:]
+                    )
+                nc.scalar.copy(
+                    weights[:, first : b + 1, b * P : (b + 1) * P],
+                    a_flip[:, :seen].rearrange("p (k j) -> p k j", j=P),
+                )
+                if b % 2 == 0:
+                    continue
+
+                j0 = (b - 1) * P
+                key_blocks = [b - 1] + [kb for kb in range(max(0, b - 1 - BACK), b + 1) if kb != b - 1]
+                att_bf = tail.tile([P, CB, CHUNK], BF16)
+                for d in range(CB):
+                    att_ps = psum_acc.tile([P, CHUNK], F32, tag="acc")
+                    for kb in key_blocks:
+                        lo = max(b - 1, kb) * P
+                        hi = (min(b, kb + BACK) + 1) * P
+                        nc.tensor.matmul(
+                            att_ps[:, lo - j0 : hi - j0],
+                            v_bf[kb][:, d * P : (d + 1) * P],
+                            weights[:, kb, lo:hi],
+                            start=(kb == key_blocks[0]),
+                            stop=(kb == key_blocks[-1]),
+                        )
+                    nc.scalar.copy(att_bf[:, d, :], att_ps[:])
+
+                z = tail.tile([P, CB, CHUNK], F32)
+                for m in range(CB):
+                    z_ps = psum_acc.tile([P, CHUNK], F32, tag="acc")
+                    for d in range(CB):
+                        nc.tensor.matmul(
+                            z_ps[:],
+                            weight_sb["wo"][:, d, m * P : (m + 1) * P],
+                            att_bf[:, d, :],
+                            start=(d == 0),
+                            stop=(d == CB - 1),
+                        )
+                    nc.vector.scalar_tensor_tensor(
+                        z[:, m, :], z_ps[:], bo_col[m], h[m][:, j0 : j0 + CHUNK], ADD, ADD
+                    )
+
+                z_bf = tail.tile([P, CB, CHUNK], BF16)
+                nc.scalar.copy(z_bf[:], z[:])
+                mu_ps = psum_stat.tile([P, CHUNK], F32, tag="stat")
+                for m in range(CB):
+                    nc.tensor.matmul(
+                        mu_ps[:], mean_w[:], z_bf[:, m, :], start=(m == 0), stop=(m == CB - 1)
+                    )
+                zc = tail.tile([P, CB, CHUNK], F32)
+                nc.vector.tensor_tensor(
+                    zc[:], z[:], mu_ps[:].unsqueeze(1).to_broadcast([P, CB, CHUNK]), SUB
+                )
+                sq_bf = tail.tile([P, CB, CHUNK], BF16)
+                nc.scalar.activation(sq_bf[:], zc[:], FUNC.Square)
+                var_ps = psum_stat.tile([P, CHUNK], F32, tag="stat")
+                for m in range(CB):
+                    nc.tensor.matmul(
+                        var_ps[:], mean_w[:], sq_bf[:, m, :], start=(m == 0), stop=(m == CB - 1)
+                    )
+                ln_var = tail.tile([P, CHUNK], F32)
+                nc.scalar.activation(ln_var[:], var_ps[:], FUNC.Ln, bias=eps_col[:])
+                rstd = tail.tile([P, CHUNK], F32)
+                nc.scalar.activation(rstd[:], ln_var[:], FUNC.Exp, scale=-0.5)
+                normed = tail.tile([P, CB, CHUNK], F32)
+                nc.vector.tensor_tensor(
+                    normed[:], zc[:], rstd[:].unsqueeze(1).to_broadcast([P, CB, CHUNK]), MULT
+                )
+                for m in range(CB):
+                    o = store.tile([P, CHUNK], F32)
+                    nc.scalar.activation(
+                        o[:], normed[:, m, :], FUNC.Identity, bias=bias_col[m], scale=gain_col[m]
+                    )
+                    nc.sync.dma_start(out[m * P : (m + 1) * P, j0 : j0 + CHUNK], o[:])

@@ -23,7 +23,9 @@ REACH = WIN * GRID + WIN
 BACK = -(-REACH // P)
 SEEN = (BACK + 1) * P
 CHUNK = 2 * P
+NCHUNK = N // CHUNK
 SHUT = 1e30
+AHEAD = 2
 
 NEAR = sum(GRID - d for d in range(1, WIN + 1))
 PAIRS = NEAR * (GRID + 2 * NEAR) + GRID * (GRID + NEAR)
@@ -36,10 +38,10 @@ def tile_autoregressivemodel_b_kernel(
     nc = tc.nc
     with (
         tc.tile_pool(name="held", bufs=1) as held,
-        tc.psum_pool(name="psum_acc", bufs=3) as psum_acc,
-        tc.psum_pool(name="psum_score", bufs=2) as psum_score,
+        tc.psum_pool(name="psum_acc", bufs=4) as psum_acc,
+        tc.psum_pool(name="psum_score", bufs=AHEAD) as psum_score,
         tc.psum_pool(name="psum_flip", bufs=1) as psum_flip,
-        tc.psum_pool(name="psum_stat", bufs=2) as psum_stat,
+        tc.psum_pool(name="psum_stat", bufs=1) as psum_stat,
     ):
         offsets = held.tile([P, N // 16], U16, name="offsets")
         nc.sync.dma_start(offsets[:], offs)
@@ -51,9 +53,9 @@ def tile_autoregressivemodel_b_kernel(
                 rows[k * CB : (k + 1) * CB, :], vec.rearrange("(c p) o -> c (p o)", p=P)
             )
 
-        weight_sb = {}
-        for name, w in (("wq", wq), ("wk", wk), ("wv", wv), ("wo", wo)):
-            weight_sb[name] = held.tile([P, CB, D], BF16, name=name + "_sb")
+        weight_sb = {
+            name: held.tile([P, CB, D], BF16, name=name + "_sb") for name in ("wq", "wk", "wv", "wo")
+        }
         bv_all = held.tile([P, D], F32, name="bv_all")
         allow_sb = [
             held.tile([P, min(SEEN, N - kb * P)], F32, name=f"allow_sb{kb}") for kb in range(NB)
@@ -61,15 +63,18 @@ def tile_autoregressivemodel_b_kernel(
         h = [held.tile([P, N], F32, name=f"h{c}") for c in range(CB)]
         h_bf = [held.tile([P, N], BF16, name=f"h_bf{c}") for c in range(CB)]
 
-        with tc.tile_pool(name="load", bufs=1) as load:
-            table_sb = [load.tile([P, WORDS], F32, name=f"table_sb{c}") for c in range(CB)]
-            pos_sb = [load.tile([P, N], F32, name=f"pos_sb{c}") for c in range(CB)]
+        with tc.tile_pool(name="lookup", bufs=1) as lookup:
+            table_sb = [lookup.tile([P, WORDS], F32, name=f"table_sb{c}") for c in range(CB)]
+            pos_sb = [lookup.tile([P, N], F32, name=f"pos_sb{c}") for c in range(CB)]
             for c in range(CB):
                 nc.sync.dma_start(table_sb[c][:], table[c * P : (c + 1) * P, :])
                 nc.sync.dma_start(pos_sb[c][:], pos[c * P : (c + 1) * P, :])
-            for name, w in (("wq", wq), ("wk", wk), ("wv", wv)):
-                nc.sync.dma_start(weight_sb[name][:], w.rearrange("(c p) d -> p c d", p=P))
-            nc.sync.dma_start(bv_all[:], bv.rearrange("d o -> (d o)").partition_broadcast(P))
+                if c == 1:
+                    for name, w in (("wq", wq), ("wk", wk), ("wv", wv)):
+                        nc.sync.dma_start(weight_sb[name][:], w.rearrange("(c p) d -> p c d", p=P))
+                    nc.sync.dma_start(
+                        bv_all[:], bv.rearrange("d o -> (d o)").partition_broadcast(P)
+                    )
             for kb in range(NB):
                 width = min(SEEN, N - kb * P)
                 nc.sync.dma_start(
@@ -78,10 +83,13 @@ def tile_autoregressivemodel_b_kernel(
             nc.sync.dma_start(weight_sb["wo"][:], wo.rearrange("(c p) d -> p c d", p=P))
 
             for c in range(CB):
-                nc.vector.tensor_tensor(
-                    h[c][:], table_sb[c][:].indirect(offsets[:]), pos_sb[c][:], ADD
-                )
-                nc.vector.tensor_copy(h_bf[c][:], h[c][:])
+                for half in range(N // HALF):
+                    span = slice(half * HALF, (half + 1) * HALF)
+                    piece = offsets[:, half * HALF // 16 : (half + 1) * HALF // 16]
+                    nc.vector.tensor_tensor(
+                        h[c][:, span], table_sb[c][:].indirect(piece), pos_sb[c][:, span], ADD
+                    )
+                    nc.vector.tensor_copy(h_bf[c][:, span], h[c][:, span])
 
         ident_f32 = held.tile([P, P], F32, name="ident_f32")
         make_identity(nc, ident_f32[:])
@@ -103,40 +111,49 @@ def tile_autoregressivemodel_b_kernel(
         q_bf = [held.tile([P, N], BF16, name=f"q_bf{d}") for d in range(CB)]
         k_bf = [held.tile([P, N], BF16, name=f"k_bf{d}") for d in range(CB)]
         v_bf = [held.tile([P, D], BF16, name=f"v_bf{i}") for i in range(NB)]
-        for half in range(N // HALF):
-            span = slice(half * HALF, (half + 1) * HALF)
-            for d in range(CB):
-                q_ps = psum_acc.tile([P, HALF], F32, tag="acc")
-                for c in range(CB):
-                    nc.tensor.matmul(
-                        q_ps[:],
-                        weight_sb["wq"][:, c, d * P : (d + 1) * P],
-                        h_bf[c][:, span],
-                        start=(c == 0),
-                        stop=(c == CB - 1),
-                    )
-                nc.scalar.copy(q_bf[d][:, span], q_ps[:])
-                k_ps = psum_acc.tile([P, HALF], F32, tag="acc")
-                for c in range(CB):
-                    nc.tensor.matmul(
-                        k_ps[:],
-                        weight_sb["wk"][:, c, d * P : (d + 1) * P],
-                        h_bf[c][:, span],
-                        start=(c == 0),
-                        stop=(c == CB - 1),
-                    )
-                nc.scalar.copy(k_bf[d][:, span], k_ps[:])
-            for i in range(half * HALF // P, (half + 1) * HALF // P):
-                v_ps = psum_acc.tile([P, D], F32, tag="acc")
-                for c in range(CB):
-                    nc.tensor.matmul(
-                        v_ps[:],
-                        h_bf[c][:, i * P : (i + 1) * P],
-                        weight_sb["wv"][:, c, :],
-                        start=(c == 0),
-                        stop=(c == CB - 1),
-                    )
-                nc.vector.tensor_tensor(v_bf[i][:], v_ps[:], bv_all[:], ADD)
+
+        qk_jobs = [(kind, d, half) for half in range(N // HALF) for d in range(CB) for kind in "qk"]
+        v_jobs = [("v", i, 0) for i in range(NB)]
+        jobs = qk_jobs + v_jobs
+
+        def project(job, blocks):
+            kind, index, half = job
+            acc = psum_acc.tile([P, HALF], F32, tag="acc")
+            for c in blocks:
+                if kind == "v":
+                    stationary = h_bf[c][:, index * P : (index + 1) * P]
+                    moving = weight_sb["wv"][:, c, :]
+                else:
+                    stationary = weight_sb["w" + kind][:, c, index * P : (index + 1) * P]
+                    moving = h_bf[c][:, half * HALF : (half + 1) * HALF]
+                nc.tensor.matmul(
+                    acc[:], stationary, moving, start=(c == blocks[0]), stop=(c == blocks[-1])
+                )
+            return acc
+
+        parked = {job: held.tile([P, HALF], F32, name="parked_%s%d%d" % job) for job in jobs}
+
+        def first_half(job):
+            acc = project(job, (0, 1))
+            if job[0] == "v":
+                nc.vector.tensor_tensor(parked[job][:], acc[:], bv_all[:], ADD)
+            else:
+                nc.scalar.copy(parked[job][:], acc[:])
+
+        def second_half(job):
+            kind, index, half = job
+            acc = project(job, (2, 3))
+            if kind == "v":
+                result = v_bf[index][:]
+            else:
+                result = (q_bf if kind == "q" else k_bf)[index][:, half * HALF : (half + 1) * HALF]
+            nc.vector.tensor_tensor(result, acc[:], parked[job][:], ADD)
+
+        for job in jobs:
+            first_half(job)
+        for job in qk_jobs[: 2 * CB]:
+            second_half(job)
+        waiting = jobs[2 * CB :]
 
         shut = [held.tile([P, SEEN], F32, name=f"shut{b}") for b in range(NB)]
         for b in range(NB):
@@ -149,32 +166,40 @@ def tile_autoregressivemodel_b_kernel(
                     allow_sb[kb][:, (b - kb) * P : (b - kb + 1) * P],
                     ident_f32[:],
                 )
-            nc.vector.tensor_scalar(shut[b][:, :seen], allow_flip[:, :seen], 1.0, SHUT, SUB, MULT)
-
-        weights = held.tile([P, NB, N], BF16, name="weights")
+            nc.scalar.activation(
+                shut[b][:, :seen], allow_flip[:, :seen], FUNC.Copy, bias=-SHUT, scale=SHUT
+            )
 
         with (
+            tc.tile_pool(name="late", bufs=1) as late,
             tc.tile_pool(name="soft", bufs=2) as soft,
             tc.tile_pool(name="tiny", bufs=4) as tiny,
             tc.tile_pool(name="tail", bufs=2) as tail,
             tc.tile_pool(name="store", bufs=4) as store,
         ):
-            for b in range(NB):
+            weights = late.tile([P, NB, N], BF16, name="weights")
+            score_ps, a = {}, {}
+
+            def scores(b):
                 first = max(0, b - BACK)
                 seen = (b + 1 - first) * P
-                score_ps = psum_score.tile([P, SEEN], F32, tag="score")
+                score_ps[b] = psum_score.tile([P, SEEN], F32, tag="score", name="score_ps")
                 for d in range(CB):
                     nc.tensor.matmul(
-                        score_ps[:, :seen],
+                        score_ps[b][:, :seen],
                         q_bf[d][:, b * P : (b + 1) * P],
                         k_bf[d][:, first * P : (b + 1) * P],
                         start=(d == 0),
                         stop=(d == CB - 1),
                     )
+
+            def softmax(b):
+                first = max(0, b - BACK)
+                seen = (b + 1 - first) * P
                 masked = soft.tile([P, SEEN], F32)
                 nc.vector.scalar_tensor_tensor(
                     masked[:, :seen],
-                    score_ps[:, :seen],
+                    score_ps[b][:, :seen],
                     1.0 / math.sqrt(D),
                     shut[b][:, :seen],
                     MULT,
@@ -191,28 +216,43 @@ def tile_autoregressivemodel_b_kernel(
                 )
                 inv_total = tiny.tile([P, 1], F32)
                 nc.vector.reciprocal(inv_total[:], total[:])
-                a = soft.tile([P, SEEN], BF16)
-                nc.vector.tensor_scalar_mul(a[:, :seen], e[:, :seen], inv_total[:])
+                a[b] = soft.tile([P, SEEN], BF16, name="a")
+                nc.scalar.activation(a[b][:, :seen], e[:, :seen], FUNC.Identity, scale=inv_total[:])
+
+            def flip(b):
+                first = max(0, b - BACK)
+                seen = (b + 1 - first) * P
                 a_flip = psum_flip.tile([P, SEEN], BF16, tag="flip")
                 for kk in range(b + 1 - first):
                     nc.tensor.transpose(
-                        a_flip[:, kk * P : (kk + 1) * P], a[:, kk * P : (kk + 1) * P], ident_bf16[:]
+                        a_flip[:, kk * P : (kk + 1) * P], a[b][:, kk * P : (kk + 1) * P], ident_bf16[:]
                     )
                 nc.scalar.copy(
                     weights[:, first : b + 1, b * P : (b + 1) * P],
                     a_flip[:, :seen].rearrange("p (k j) -> p k j", j=P),
                 )
-                if b % 2 == 0:
-                    continue
 
-                j0 = (b - 1) * P
-                key_blocks = [b - 1] + [kb for kb in range(max(0, b - 1 - BACK), b + 1) if kb != b - 1]
-                att_bf = tail.tile([P, CB, CHUNK], BF16)
+            for b in range(AHEAD):
+                scores(b)
+            for b in range(NB):
+                for job in waiting[3 * b : 3 * b + 3]:
+                    second_half(job)
+                softmax(b)
+                if b + AHEAD < NB:
+                    scores(b + AHEAD)
+                flip(b)
+
+            att_bf, z, z_bf, zc, sq_bf = {}, {}, {}, {}, {}
+
+            def weighted_sum(c):
+                j0, b0, b1 = c * CHUNK, 2 * c, 2 * c + 1
+                key_blocks = [b0] + [kb for kb in range(max(0, b0 - BACK), b1 + 1) if kb != b0]
+                att_bf[c] = [tail.tile([P, CHUNK], BF16, name=f"att_bf{d}") for d in range(CB)]
                 for d in range(CB):
                     att_ps = psum_acc.tile([P, CHUNK], F32, tag="acc")
                     for kb in key_blocks:
-                        lo = max(b - 1, kb) * P
-                        hi = (min(b, kb + BACK) + 1) * P
+                        lo = max(b0, kb) * P
+                        hi = (min(b1, kb + BACK) + 1) * P
                         nc.tensor.matmul(
                             att_ps[:, lo - j0 : hi - j0],
                             v_bf[kb][:, d * P : (d + 1) * P],
@@ -220,52 +260,63 @@ def tile_autoregressivemodel_b_kernel(
                             start=(kb == key_blocks[0]),
                             stop=(kb == key_blocks[-1]),
                         )
-                    nc.scalar.copy(att_bf[:, d, :], att_ps[:])
+                    nc.scalar.copy(att_bf[c][d][:], att_ps[:])
 
-                z = tail.tile([P, CB, CHUNK], F32)
+            def residual(c):
+                j0 = c * CHUNK
+                z[c] = [tail.tile([P, CHUNK], F32, name=f"z{m}") for m in range(CB)]
+                z_bf[c] = [tail.tile([P, CHUNK], BF16, name=f"z_bf{m}") for m in range(CB)]
                 for m in range(CB):
                     z_ps = psum_acc.tile([P, CHUNK], F32, tag="acc")
                     for d in range(CB):
                         nc.tensor.matmul(
                             z_ps[:],
                             weight_sb["wo"][:, d, m * P : (m + 1) * P],
-                            att_bf[:, d, :],
+                            att_bf[c][d][:],
                             start=(d == 0),
                             stop=(d == CB - 1),
                         )
                     nc.vector.scalar_tensor_tensor(
-                        z[:, m, :], z_ps[:], bo_col[m], h[m][:, j0 : j0 + CHUNK], ADD, ADD
+                        z[c][m][:], z_ps[:], bo_col[m], h[m][:, j0 : j0 + CHUNK], ADD, ADD
                     )
+                    nc.scalar.copy(z_bf[c][m][:], z[c][m][:])
 
-                z_bf = tail.tile([P, CB, CHUNK], BF16)
-                nc.scalar.copy(z_bf[:], z[:])
+            def centre(c):
                 mu_ps = psum_stat.tile([P, CHUNK], F32, tag="stat")
                 for m in range(CB):
                     nc.tensor.matmul(
-                        mu_ps[:], mean_w[:], z_bf[:, m, :], start=(m == 0), stop=(m == CB - 1)
+                        mu_ps[:], mean_w[:], z_bf[c][m][:], start=(m == 0), stop=(m == CB - 1)
                     )
-                zc = tail.tile([P, CB, CHUNK], F32)
-                nc.vector.tensor_tensor(
-                    zc[:], z[:], mu_ps[:].unsqueeze(1).to_broadcast([P, CB, CHUNK]), SUB
-                )
-                sq_bf = tail.tile([P, CB, CHUNK], BF16)
-                nc.scalar.activation(sq_bf[:], zc[:], FUNC.Square)
+                zc[c] = [tail.tile([P, CHUNK], F32, name=f"zc{m}") for m in range(CB)]
+                sq_bf[c] = [tail.tile([P, CHUNK], BF16, name=f"sq_bf{m}") for m in range(CB)]
+                for m in range(CB):
+                    nc.vector.tensor_tensor(zc[c][m][:], z[c][m][:], mu_ps[:], SUB)
+                    nc.scalar.activation(sq_bf[c][m][:], zc[c][m][:], FUNC.Square)
+
+            def normalise(c):
+                j0 = c * CHUNK
                 var_ps = psum_stat.tile([P, CHUNK], F32, tag="stat")
                 for m in range(CB):
                     nc.tensor.matmul(
-                        var_ps[:], mean_w[:], sq_bf[:, m, :], start=(m == 0), stop=(m == CB - 1)
+                        var_ps[:], mean_w[:], sq_bf[c][m][:], start=(m == 0), stop=(m == CB - 1)
                     )
-                ln_var = tail.tile([P, CHUNK], F32)
-                nc.scalar.activation(ln_var[:], var_ps[:], FUNC.Ln, bias=eps_col[:])
                 rstd = tail.tile([P, CHUNK], F32)
-                nc.scalar.activation(rstd[:], ln_var[:], FUNC.Exp, scale=-0.5)
-                normed = tail.tile([P, CB, CHUNK], F32)
-                nc.vector.tensor_tensor(
-                    normed[:], zc[:], rstd[:].unsqueeze(1).to_broadcast([P, CB, CHUNK]), MULT
-                )
+                nc.scalar.activation(rstd[:], var_ps[:], FUNC.Abs_reciprocal_sqrt, bias=eps_col[:])
                 for m in range(CB):
+                    normed = tail.tile([P, CHUNK], F32)
+                    nc.vector.tensor_tensor(normed[:], zc[c][m][:], rstd[:], MULT)
                     o = store.tile([P, CHUNK], F32)
                     nc.scalar.activation(
-                        o[:], normed[:, m, :], FUNC.Identity, bias=bias_col[m], scale=gain_col[m]
+                        o[:], normed[:], FUNC.Identity, bias=bias_col[m], scale=gain_col[m]
                     )
                     nc.sync.dma_start(out[m * P : (m + 1) * P, j0 : j0 + CHUNK], o[:])
+
+            for c in range(NCHUNK + 1):
+                if c < NCHUNK:
+                    weighted_sum(c)
+                if c > 0:
+                    centre(c - 1)
+                if c < NCHUNK:
+                    residual(c)
+                if c > 0:
+                    normalise(c - 1)

@@ -24,6 +24,7 @@ BACK = -(-REACH // P)
 SEEN = (BACK + 1) * P
 CHUNK = 2 * P
 NCHUNK = N // CHUNK
+SCALE = 1.0 / math.sqrt(D)
 SHUT = 1e30
 AHEAD = 2
 
@@ -57,9 +58,8 @@ def tile_autoregressivemodel_b_kernel(
             name: held.tile([P, CB, D], BF16, name=name + "_sb") for name in ("wq", "wk", "wv", "wo")
         }
         bv_all = held.tile([P, D], F32, name="bv_all")
-        allow_sb = [
-            held.tile([P, min(SEEN, N - kb * P)], F32, name=f"allow_sb{kb}") for kb in range(NB)
-        ]
+        served = [min(SEEN, N - kb * P) for kb in range(NB)]
+        allow_sb = [held.tile([P, served[kb]], F32, name=f"allow_sb{kb}") for kb in range(NB)]
         h = [held.tile([P, N], F32, name=f"h{c}") for c in range(CB)]
         h_bf = [held.tile([P, N], BF16, name=f"h_bf{c}") for c in range(CB)]
 
@@ -76,9 +76,8 @@ def tile_autoregressivemodel_b_kernel(
                         bv_all[:], bv.rearrange("d o -> (d o)").partition_broadcast(P)
                     )
             for kb in range(NB):
-                width = min(SEEN, N - kb * P)
                 nc.sync.dma_start(
-                    allow_sb[kb][:], allow[kb * P : (kb + 1) * P, kb * P : kb * P + width]
+                    allow_sb[kb][:], allow[kb * P : (kb + 1) * P, kb * P : kb * P + served[kb]]
                 )
             nc.sync.dma_start(weight_sb["wo"][:], wo.rearrange("(c p) d -> p c d", p=P))
 
@@ -153,22 +152,11 @@ def tile_autoregressivemodel_b_kernel(
             first_half(job)
         for job in qk_jobs[: 2 * CB]:
             second_half(job)
-        waiting = jobs[2 * CB :]
+        late_qk_jobs = qk_jobs[2 * CB :]
 
-        shut = [held.tile([P, SEEN], F32, name=f"shut{b}") for b in range(NB)]
-        for b in range(NB):
-            first = max(0, b - BACK)
-            seen = (b + 1 - first) * P
-            allow_flip = psum_score.tile([P, SEEN], F32, tag="score")
-            for kb in range(first, b + 1):
-                nc.tensor.transpose(
-                    allow_flip[:, (kb - first) * P : (kb - first + 1) * P],
-                    allow_sb[kb][:, (b - kb) * P : (b - kb + 1) * P],
-                    ident_f32[:],
-                )
-            nc.scalar.activation(
-                shut[b][:, :seen], allow_flip[:, :seen], FUNC.Copy, bias=-SHUT, scale=SHUT
-            )
+        shut = [held.tile([P, served[kb]], BF16, name=f"shut{kb}") for kb in range(NB)]
+        for kb in range(NB):
+            nc.scalar.activation(shut[kb][:], allow_sb[kb][:], FUNC.Copy, bias=-SHUT, scale=SHUT)
 
         with (
             tc.tile_pool(name="late", bufs=1) as late,
@@ -190,29 +178,33 @@ def tile_autoregressivemodel_b_kernel(
                         q_bf[d][:, b * P : (b + 1) * P],
                         k_bf[d][:, first * P : (b + 1) * P],
                         start=(d == 0),
-                        stop=(d == CB - 1),
+                        stop=False,
+                    )
+                for kb in range(first, b + 1):
+                    nc.tensor.matmul(
+                        score_ps[b][:, (kb - first) * P : (kb - first + 1) * P],
+                        shut[kb][:, (b - kb) * P : (b - kb + 1) * P],
+                        ident_bf16[:],
+                        start=False,
+                        stop=(kb == b),
                     )
 
             def softmax(b):
                 first = max(0, b - BACK)
                 seen = (b + 1 - first) * P
-                masked = soft.tile([P, SEEN], F32)
-                nc.vector.scalar_tensor_tensor(
-                    masked[:, :seen],
-                    score_ps[b][:, :seen],
-                    1.0 / math.sqrt(D),
-                    shut[b][:, :seen],
-                    MULT,
-                    ADD,
-                )
                 top = tiny.tile([P, 1], F32)
-                nc.vector.reduce_max(top[:], masked[:, :seen], axis=ALONG_FREE)
+                nc.vector.reduce_max(top[:], score_ps[b][:, :seen], axis=ALONG_FREE)
                 neg_top = tiny.tile([P, 1], F32)
-                nc.vector.tensor_scalar_mul(neg_top[:], top[:], -1.0)
+                nc.vector.tensor_scalar_mul(neg_top[:], top[:], -SCALE)
                 e = soft.tile([P, SEEN], F32)
                 total = tiny.tile([P, 1], F32)
                 nc.scalar.activation(
-                    e[:, :seen], masked[:, :seen], FUNC.Exp, bias=neg_top[:], accum_out=total[:]
+                    e[:, :seen],
+                    score_ps[b][:, :seen],
+                    FUNC.Exp,
+                    bias=neg_top[:],
+                    scale=SCALE,
+                    accum_out=total[:],
                 )
                 inv_total = tiny.tile([P, 1], F32)
                 nc.vector.reciprocal(inv_total[:], total[:])
@@ -235,12 +227,14 @@ def tile_autoregressivemodel_b_kernel(
             for b in range(AHEAD):
                 scores(b)
             for b in range(NB):
-                for job in waiting[3 * b : 3 * b + 3]:
+                for job in late_qk_jobs[3 * b : 3 * b + 3]:
                     second_half(job)
                 softmax(b)
                 if b + AHEAD < NB:
                     scores(b + AHEAD)
                 flip(b)
+            for job in v_jobs:
+                second_half(job)
 
             att_bf, z, z_bf, zc, sq_bf = {}, {}, {}, {}, {}
 
@@ -279,7 +273,7 @@ def tile_autoregressivemodel_b_kernel(
                     nc.vector.scalar_tensor_tensor(
                         z[c][m][:], z_ps[:], bo_col[m], h[m][:, j0 : j0 + CHUNK], ADD, ADD
                     )
-                    nc.scalar.copy(z_bf[c][m][:], z[c][m][:])
+                    nc.vector.tensor_copy(z_bf[c][m][:], z[c][m][:])
 
             def centre(c):
                 mu_ps = psum_stat.tile([P, CHUNK], F32, tag="stat")

@@ -49,7 +49,7 @@ def tile_autoregressivemodel_b_kernel(
 
         rows = held.tile([P, P], F32, name="rows")
         nc.vector.memset(rows[:], 0.0)
-        for k, vec in enumerate((bo, ln_gain, ln_bias)):
+        for k, vec in enumerate((bo, ln_gain, ln_bias, bv)):
             nc.sync.dma_start(
                 rows[k * CB : (k + 1) * CB, :], vec.rearrange("(c p) o -> c (p o)", p=P)
             )
@@ -57,7 +57,10 @@ def tile_autoregressivemodel_b_kernel(
         weight_sb = {
             name: held.tile([P, CB, D], BF16, name=name + "_sb") for name in ("wq", "wk", "wv", "wo")
         }
-        bv_all = held.tile([P, D], F32, name="bv_all")
+
+        def load_weight(name, w):
+            nc.sync.dma_start(weight_sb[name][:], w.rearrange("(c p) d -> p c d", p=P))
+
         served = [min(SEEN, N - kb * P) for kb in range(NB)]
         allow_sb = [held.tile([P, served[kb]], F32, name=f"allow_sb{kb}") for kb in range(NB)]
         h = [held.tile([P, N], F32, name=f"h{c}") for c in range(CB)]
@@ -66,20 +69,74 @@ def tile_autoregressivemodel_b_kernel(
         with tc.tile_pool(name="lookup", bufs=1) as lookup:
             table_sb = [lookup.tile([P, WORDS], F32, name=f"table_sb{c}") for c in range(CB)]
             pos_sb = [lookup.tile([P, N], F32, name=f"pos_sb{c}") for c in range(CB)]
+            load_weight("wv", wv)
+            load_weight("wo", wo)
             for c in range(CB):
                 nc.sync.dma_start(table_sb[c][:], table[c * P : (c + 1) * P, :])
                 nc.sync.dma_start(pos_sb[c][:], pos[c * P : (c + 1) * P, :])
-                if c == 1:
-                    for name, w in (("wq", wq), ("wk", wk), ("wv", wv)):
-                        nc.sync.dma_start(weight_sb[name][:], w.rearrange("(c p) d -> p c d", p=P))
-                    nc.sync.dma_start(
-                        bv_all[:], bv.rearrange("d o -> (d o)").partition_broadcast(P)
-                    )
+                if c == 0:
+                    load_weight("wq", wq)
+                    load_weight("wk", wk)
             for kb in range(NB):
                 nc.sync.dma_start(
                     allow_sb[kb][:], allow[kb * P : (kb + 1) * P, kb * P : kb * P + served[kb]]
                 )
-            nc.sync.dma_start(weight_sb["wo"][:], wo.rearrange("(c p) d -> p c d", p=P))
+
+            ident_f32 = held.tile([P, P], F32, name="ident_f32")
+            make_identity(nc, ident_f32[:])
+            ident_bf16 = held.tile([P, P], BF16, name="ident_bf16")
+            nc.vector.tensor_copy(ident_bf16[:], ident_f32[:])
+            ones_bf16 = held.tile([P, P], BF16, name="ones_bf16")
+            nc.vector.memset(ones_bf16[:], 1.0)
+            mean_w = held.tile([P, P], BF16, name="mean_w")
+            nc.vector.memset(mean_w[:], 1.0 / D)
+            eps_col = held.tile([P, 1], F32, name="eps_col")
+            nc.vector.memset(eps_col[:], EPS)
+
+            cols_ps = psum_flip.tile([P, P], F32, tag="flip")
+            nc.tensor.transpose(cols_ps[:], rows[:], ident_f32[:])
+            cols = held.tile([P, 4 * CB], F32, name="cols")
+            nc.vector.tensor_copy(cols[:], cols_ps[:, : 4 * CB])
+            bo_col = [cols[:, m : m + 1] for m in range(CB)]
+            gain_col = [cols[:, CB + m : CB + m + 1] for m in range(CB)]
+            bias_col = [cols[:, 2 * CB + m : 2 * CB + m + 1] for m in range(CB)]
+            bv_col = [cols[:, 3 * CB + d : 3 * CB + d + 1] for d in range(CB)]
+
+            wv_flip = held.tile([P, CB, D], BF16, name="wv_flip")
+            for d in range(CB):
+                flip_ps = psum_flip.tile([P, D], BF16, tag="flip")
+                for c in range(CB):
+                    nc.tensor.transpose(
+                        flip_ps[:, c * P : (c + 1) * P],
+                        weight_sb["wv"][:, c, d * P : (d + 1) * P],
+                        ident_bf16[:],
+                    )
+                nc.scalar.copy(wv_flip[:, d, :], flip_ps[:])
+            wvo = held.tile([P, CB, D], BF16, name="wvo")
+            for c in range(CB):
+                wvo_ps = psum_acc.tile([P, D], F32, tag="acc")
+                for d in range(CB):
+                    nc.tensor.matmul(
+                        wvo_ps[:],
+                        wv_flip[:, d, c * P : (c + 1) * P],
+                        weight_sb["wo"][:, d, :],
+                        start=(d == 0),
+                        stop=(d == CB - 1),
+                    )
+                nc.scalar.copy(wvo[:, c, :], wvo_ps[:])
+            bv_wide = held.tile([P, CB, P], BF16, name="bv_wide")
+            bvo_ps = psum_acc.tile([P, D], F32, tag="acc")
+            for d in range(CB):
+                nc.vector.tensor_scalar_mul(bv_wide[:, d, :], ones_bf16[:], bv_col[d])
+                nc.tensor.matmul(
+                    bvo_ps[:],
+                    bv_wide[:, d, :],
+                    weight_sb["wo"][:, d, :],
+                    start=(d == 0),
+                    stop=(d == CB - 1),
+                )
+            bvo_all = held.tile([P, D], F32, name="bvo_all")
+            nc.scalar.copy(bvo_all[:], bvo_ps[:])
 
             for c in range(CB):
                 for half in range(N // HALF):
@@ -90,38 +147,21 @@ def tile_autoregressivemodel_b_kernel(
                     )
                     nc.vector.tensor_copy(h_bf[c][:, span], h[c][:, span])
 
-        ident_f32 = held.tile([P, P], F32, name="ident_f32")
-        make_identity(nc, ident_f32[:])
-        ident_bf16 = held.tile([P, P], BF16, name="ident_bf16")
-        nc.vector.tensor_copy(ident_bf16[:], ident_f32[:])
-        mean_w = held.tile([P, P], BF16, name="mean_w")
-        nc.vector.memset(mean_w[:], 1.0 / D)
-        eps_col = held.tile([P, 1], F32, name="eps_col")
-        nc.vector.memset(eps_col[:], EPS)
-
-        cols_ps = psum_flip.tile([P, P], F32, tag="flip")
-        nc.tensor.transpose(cols_ps[:], rows[:], ident_f32[:])
-        cols = held.tile([P, 3 * CB], F32, name="cols")
-        nc.vector.tensor_copy(cols[:], cols_ps[:, : 3 * CB])
-        bo_col = [cols[:, m : m + 1] for m in range(CB)]
-        gain_col = [cols[:, CB + m : CB + m + 1] for m in range(CB)]
-        bias_col = [cols[:, 2 * CB + m : 2 * CB + m + 1] for m in range(CB)]
-
         q_bf = [held.tile([P, N], BF16, name=f"q_bf{d}") for d in range(CB)]
         k_bf = [held.tile([P, N], BF16, name=f"k_bf{d}") for d in range(CB)]
-        v_bf = [held.tile([P, D], BF16, name=f"v_bf{i}") for i in range(NB)]
+        u_bf = [held.tile([P, D], BF16, name=f"u_bf{i}") for i in range(NB)]
 
         qk_jobs = [(kind, d, half) for half in range(N // HALF) for d in range(CB) for kind in "qk"]
-        v_jobs = [("v", i, 0) for i in range(NB)]
-        jobs = qk_jobs + v_jobs
+        u_jobs = [("u", i, 0) for i in range(NB)]
+        jobs = qk_jobs + u_jobs
 
         def project(job, blocks):
             kind, index, half = job
             acc = psum_acc.tile([P, HALF], F32, tag="acc")
             for c in blocks:
-                if kind == "v":
+                if kind == "u":
                     stationary = h_bf[c][:, index * P : (index + 1) * P]
-                    moving = weight_sb["wv"][:, c, :]
+                    moving = wvo[:, c, :]
                 else:
                     stationary = weight_sb["w" + kind][:, c, index * P : (index + 1) * P]
                     moving = h_bf[c][:, half * HALF : (half + 1) * HALF]
@@ -134,16 +174,16 @@ def tile_autoregressivemodel_b_kernel(
 
         def first_half(job):
             acc = project(job, (0, 1))
-            if job[0] == "v":
-                nc.vector.tensor_tensor(parked[job][:], acc[:], bv_all[:], ADD)
+            if job[0] == "u":
+                nc.vector.tensor_tensor(parked[job][:], acc[:], bvo_all[:], ADD)
             else:
                 nc.scalar.copy(parked[job][:], acc[:])
 
         def second_half(job):
             kind, index, half = job
             acc = project(job, (2, 3))
-            if kind == "v":
-                result = v_bf[index][:]
+            if kind == "u":
+                result = u_bf[index][:]
             else:
                 result = (q_bf if kind == "q" else k_bf)[index][:, half * HALF : (half + 1) * HALF]
             nc.vector.tensor_tensor(result, acc[:], parked[job][:], ADD)
@@ -162,7 +202,7 @@ def tile_autoregressivemodel_b_kernel(
             tc.tile_pool(name="late", bufs=1) as late,
             tc.tile_pool(name="soft", bufs=2) as soft,
             tc.tile_pool(name="tiny", bufs=4) as tiny,
-            tc.tile_pool(name="tail", bufs=2) as tail,
+            tc.tile_pool(name="tail", bufs=3) as tail,
             tc.tile_pool(name="store", bufs=4) as store,
         ):
             weights = late.tile([P, NB, N], BF16, name="weights")
@@ -233,42 +273,27 @@ def tile_autoregressivemodel_b_kernel(
                 if b + AHEAD < NB:
                     scores(b + AHEAD)
                 flip(b)
-            for job in v_jobs:
+            for job in u_jobs:
                 second_half(job)
 
-            att_bf, z, z_bf, zc, sq_bf = {}, {}, {}, {}, {}
+            z, z_bf, zc, sq_bf = {}, {}, {}, {}
 
             def weighted_sum(c):
                 j0, b0, b1 = c * CHUNK, 2 * c, 2 * c + 1
                 key_blocks = [b0] + [kb for kb in range(max(0, b0 - BACK), b1 + 1) if kb != b0]
-                att_bf[c] = [tail.tile([P, CHUNK], BF16, name=f"att_bf{d}") for d in range(CB)]
-                for d in range(CB):
-                    att_ps = psum_acc.tile([P, CHUNK], F32, tag="acc")
-                    for kb in key_blocks:
-                        lo = max(b0, kb) * P
-                        hi = (min(b1, kb + BACK) + 1) * P
-                        nc.tensor.matmul(
-                            att_ps[:, lo - j0 : hi - j0],
-                            v_bf[kb][:, d * P : (d + 1) * P],
-                            weights[:, kb, lo:hi],
-                            start=(kb == key_blocks[0]),
-                            stop=(kb == key_blocks[-1]),
-                        )
-                    nc.scalar.copy(att_bf[c][d][:], att_ps[:])
-
-            def residual(c):
-                j0 = c * CHUNK
                 z[c] = [tail.tile([P, CHUNK], F32, name=f"z{m}") for m in range(CB)]
                 z_bf[c] = [tail.tile([P, CHUNK], BF16, name=f"z_bf{m}") for m in range(CB)]
                 for m in range(CB):
                     z_ps = psum_acc.tile([P, CHUNK], F32, tag="acc")
-                    for d in range(CB):
+                    for kb in key_blocks:
+                        lo = max(b0, kb) * P
+                        hi = (min(b1, kb + BACK) + 1) * P
                         nc.tensor.matmul(
-                            z_ps[:],
-                            weight_sb["wo"][:, d, m * P : (m + 1) * P],
-                            att_bf[c][d][:],
-                            start=(d == 0),
-                            stop=(d == CB - 1),
+                            z_ps[:, lo - j0 : hi - j0],
+                            u_bf[kb][:, m * P : (m + 1) * P],
+                            weights[:, kb, lo:hi],
+                            start=(kb == key_blocks[0]),
+                            stop=(kb == key_blocks[-1]),
                         )
                     nc.vector.scalar_tensor_tensor(
                         z[c][m][:], z_ps[:], bo_col[m], h[m][:, j0 : j0 + CHUNK], ADD, ADD
@@ -305,12 +330,10 @@ def tile_autoregressivemodel_b_kernel(
                     )
                     nc.sync.dma_start(out[m * P : (m + 1) * P, j0 : j0 + CHUNK], o[:])
 
-            for c in range(NCHUNK + 1):
+            for c in range(NCHUNK + 2):
                 if c < NCHUNK:
                     weighted_sum(c)
-                if c > 0:
+                if 0 <= c - 1 < NCHUNK:
                     centre(c - 1)
-                if c < NCHUNK:
-                    residual(c)
-                if c > 0:
-                    normalise(c - 1)
+                if c - 2 >= 0:
+                    normalise(c - 2)

@@ -54,11 +54,9 @@ def tile_autoregressivemodel_b_kernel(
                 rows[k * CB : (k + 1) * CB, :], vec.rearrange("(c p) o -> c (p o)", p=P)
             )
 
-        weight_sb = {
-            name: held.tile([P, CB, D], BF16, name=name + "_sb") for name in ("wq", "wk", "wv", "wo")
-        }
-
-        def load_weight(name, w):
+        weight_sb = {}
+        for name, w in (("wq", wq), ("wk", wk), ("wv", wv), ("wo", wo)):
+            weight_sb[name] = held.tile([P, CB, D], BF16, name=name + "_sb")
             nc.sync.dma_start(weight_sb[name][:], w.rearrange("(c p) d -> p c d", p=P))
 
         served = [min(SEEN, N - kb * P) for kb in range(NB)]
@@ -69,14 +67,9 @@ def tile_autoregressivemodel_b_kernel(
         with tc.tile_pool(name="lookup", bufs=1) as lookup:
             table_sb = [lookup.tile([P, WORDS], F32, name=f"table_sb{c}") for c in range(CB)]
             pos_sb = [lookup.tile([P, N], F32, name=f"pos_sb{c}") for c in range(CB)]
-            load_weight("wv", wv)
-            load_weight("wo", wo)
             for c in range(CB):
-                nc.sync.dma_start(table_sb[c][:], table[c * P : (c + 1) * P, :])
                 nc.sync.dma_start(pos_sb[c][:], pos[c * P : (c + 1) * P, :])
-                if c == 0:
-                    load_weight("wq", wq)
-                    load_weight("wk", wk)
+                nc.sync.dma_start(table_sb[c][:], table[c * P : (c + 1) * P, :])
             for kb in range(NB):
                 nc.sync.dma_start(
                     allow_sb[kb][:], allow[kb * P : (kb + 1) * P, kb * P : kb * P + served[kb]]
@@ -86,57 +79,88 @@ def tile_autoregressivemodel_b_kernel(
             make_identity(nc, ident_f32[:])
             ident_bf16 = held.tile([P, P], BF16, name="ident_bf16")
             nc.vector.tensor_copy(ident_bf16[:], ident_f32[:])
-            ones_bf16 = held.tile([P, P], BF16, name="ones_bf16")
-            nc.vector.memset(ones_bf16[:], 1.0)
             mean_w = held.tile([P, P], BF16, name="mean_w")
             nc.vector.memset(mean_w[:], 1.0 / D)
+            mean_w_f32 = held.tile([P, P], F32, name="mean_w_f32")
+            nc.vector.memset(mean_w_f32[:], 1.0 / D)
             eps_col = held.tile([P, 1], F32, name="eps_col")
             nc.vector.memset(eps_col[:], EPS)
+            warm = held.tile([P, 1], F32, name="warm")
+            nc.scalar.activation(warm[:], eps_col[:], FUNC.Exp)
 
             cols_ps = psum_flip.tile([P, P], F32, tag="flip")
             nc.tensor.transpose(cols_ps[:], rows[:], ident_f32[:])
             cols = held.tile([P, 4 * CB], F32, name="cols")
             nc.vector.tensor_copy(cols[:], cols_ps[:, : 4 * CB])
-            bo_col = [cols[:, m : m + 1] for m in range(CB)]
             gain_col = [cols[:, CB + m : CB + m + 1] for m in range(CB)]
             bias_col = [cols[:, 2 * CB + m : 2 * CB + m + 1] for m in range(CB)]
-            bv_col = [cols[:, 3 * CB + d : 3 * CB + d + 1] for d in range(CB)]
 
-            wv_flip = held.tile([P, CB, D], BF16, name="wv_flip")
-            for d in range(CB):
-                flip_ps = psum_flip.tile([P, D], BF16, tag="flip")
-                for c in range(CB):
-                    nc.tensor.transpose(
-                        flip_ps[:, c * P : (c + 1) * P],
-                        weight_sb["wv"][:, c, d * P : (d + 1) * P],
-                        ident_bf16[:],
-                    )
-                nc.scalar.copy(wv_flip[:, d, :], flip_ps[:])
-            wvo = held.tile([P, CB, D], BF16, name="wvo")
-            for c in range(CB):
-                wvo_ps = psum_acc.tile([P, D], F32, tag="acc")
+            def flipped(name):
+                w_flip = held.tile([P, CB, D], BF16, name=name + "_flip")
+                for d in range(CB):
+                    flip_ps = psum_acc.tile([P, D], BF16, tag="acc")
+                    for c in range(CB):
+                        nc.tensor.transpose(
+                            flip_ps[:, c * P : (c + 1) * P],
+                            weight_sb[name][:, c, d * P : (d + 1) * P],
+                            ident_bf16[:],
+                        )
+                    if d % 2 == 0:
+                        nc.scalar.copy(w_flip[:, d, :], flip_ps[:])
+                    else:
+                        nc.vector.tensor_copy(w_flip[:, d, :], flip_ps[:])
+                return w_flip
+
+            def merged(row_block, left_flip, right):
+                product_ps = psum_acc.tile([P, D], F32, tag="acc", name="product_ps")
                 for d in range(CB):
                     nc.tensor.matmul(
-                        wvo_ps[:],
-                        wv_flip[:, d, c * P : (c + 1) * P],
-                        weight_sb["wo"][:, d, :],
+                        product_ps[:],
+                        left_flip[:, d, row_block * P : (row_block + 1) * P],
+                        right[:, d, :],
                         start=(d == 0),
                         stop=(d == CB - 1),
                     )
-                nc.scalar.copy(wvo[:, c, :], wvo_ps[:])
-            bv_wide = held.tile([P, CB, P], BF16, name="bv_wide")
-            bvo_ps = psum_acc.tile([P, D], F32, tag="acc")
-            for d in range(CB):
-                nc.vector.tensor_scalar_mul(bv_wide[:, d, :], ones_bf16[:], bv_col[d])
-                nc.tensor.matmul(
-                    bvo_ps[:],
-                    bv_wide[:, d, :],
-                    weight_sb["wo"][:, d, :],
-                    start=(d == 0),
-                    stop=(d == CB - 1),
+                return product_ps
+
+            def centred_copy(result, product_ps, name):
+                neg_mean = held.tile([P, 1], F32, name="neg_mean_" + name)
+                nc.vector.reduce_sum(neg_mean[:], product_ps[:], axis=ALONG_FREE)
+                nc.vector.tensor_scalar_mul(neg_mean[:], neg_mean[:], -1.0 / D)
+                nc.scalar.activation(result, product_ps[:], FUNC.Identity, bias=neg_mean[:])
+
+            wq_flip = flipped("wq")
+            wk_flip = flipped("wk")
+            wqk = held.tile([P, CB, D], BF16, name="wqk")
+            for c2 in range(CB):
+                nc.scalar.activation(
+                    wqk[:, c2, :], merged(c2, wq_flip, wk_flip)[:], FUNC.Copy, scale=SCALE
                 )
-            bvo_all = held.tile([P, D], F32, name="bvo_all")
-            nc.scalar.copy(bvo_all[:], bvo_ps[:])
+            wv_flip = flipped("wv")
+            wvo = held.tile([P, CB, D], BF16, name="wvo")
+            for c in range(CB):
+                centred_copy(wvo[:, c, :], merged(c, wv_flip, weight_sb["wo"]), f"wvo{c}")
+
+            bv_bf = held.tile([P, CB], BF16, name="bv_bf")
+            nc.vector.tensor_copy(bv_bf[:], cols[:, 3 * CB : 4 * CB])
+            bvo_ps = psum_flip.tile([P, CB], F32, tag="flip")
+            for m in range(CB):
+                for d in range(CB):
+                    nc.tensor.matmul(
+                        bvo_ps[:, m : m + 1],
+                        weight_sb["wo"][:, d, m * P : (m + 1) * P],
+                        bv_bf[:, d : d + 1],
+                        start=(d == 0),
+                        stop=(d == CB - 1),
+                    )
+            b_col = held.tile([P, CB], F32, name="b_col")
+            nc.vector.tensor_tensor(b_col[:], bvo_ps[:], cols[:, :CB], ADD)
+            b_sum_ps = psum_flip.tile([P, CB], F32, tag="flip")
+            nc.tensor.matmul(b_sum_ps[:], mean_w_f32[:], b_col[:])
+            b_mean = held.tile([P, 1], F32, name="b_mean")
+            nc.vector.reduce_sum(b_mean[:], b_sum_ps[:], axis=ALONG_FREE)
+            b_centred = held.tile([P, CB], F32, name="b_centred")
+            nc.vector.tensor_scalar_sub(b_centred[:], b_col[:], b_mean[:])
 
             for c in range(CB):
                 for half in range(N // HALF):
@@ -147,13 +171,11 @@ def tile_autoregressivemodel_b_kernel(
                     )
                     nc.vector.tensor_copy(h_bf[c][:, span], h[c][:, span])
 
-        q_bf = [held.tile([P, N], BF16, name=f"q_bf{d}") for d in range(CB)]
-        k_bf = [held.tile([P, N], BF16, name=f"k_bf{d}") for d in range(CB)]
+        g_bf = [held.tile([P, N], BF16, name=f"g_bf{c}") for c in range(CB)]
         u_bf = [held.tile([P, D], BF16, name=f"u_bf{i}") for i in range(NB)]
 
-        qk_jobs = [(kind, d, half) for half in range(N // HALF) for d in range(CB) for kind in "qk"]
+        g_jobs = [("g", c, half) for half in range(N // HALF) for c in range(CB)]
         u_jobs = [("u", i, 0) for i in range(NB)]
-        jobs = qk_jobs + u_jobs
 
         def project(job, blocks):
             kind, index, half = job
@@ -163,21 +185,17 @@ def tile_autoregressivemodel_b_kernel(
                     stationary = h_bf[c][:, index * P : (index + 1) * P]
                     moving = wvo[:, c, :]
                 else:
-                    stationary = weight_sb["w" + kind][:, c, index * P : (index + 1) * P]
+                    stationary = wqk[:, c, index * P : (index + 1) * P]
                     moving = h_bf[c][:, half * HALF : (half + 1) * HALF]
                 nc.tensor.matmul(
                     acc[:], stationary, moving, start=(c == blocks[0]), stop=(c == blocks[-1])
                 )
             return acc
 
-        parked = {job: held.tile([P, HALF], F32, name="parked_%s%d%d" % job) for job in jobs}
+        parked = {job: held.tile([P, HALF], F32, name="parked_%s%d%d" % job) for job in g_jobs + u_jobs}
 
         def first_half(job):
-            acc = project(job, (0, 1))
-            if job[0] == "u":
-                nc.vector.tensor_tensor(parked[job][:], acc[:], bvo_all[:], ADD)
-            else:
-                nc.scalar.copy(parked[job][:], acc[:])
+            nc.scalar.copy(parked[job][:], project(job, (0, 1))[:])
 
         def second_half(job):
             kind, index, half = job
@@ -185,39 +203,49 @@ def tile_autoregressivemodel_b_kernel(
             if kind == "u":
                 result = u_bf[index][:]
             else:
-                result = (q_bf if kind == "q" else k_bf)[index][:, half * HALF : (half + 1) * HALF]
+                result = g_bf[index][:, half * HALF : (half + 1) * HALF]
             nc.vector.tensor_tensor(result, acc[:], parked[job][:], ADD)
 
-        for job in jobs:
+        for job in g_jobs + u_jobs:
             first_half(job)
-        for job in qk_jobs[: 2 * CB]:
-            second_half(job)
-        late_qk_jobs = qk_jobs[2 * CB :]
 
         shut = [held.tile([P, served[kb]], BF16, name=f"shut{kb}") for kb in range(NB)]
         for kb in range(NB):
-            nc.scalar.activation(shut[kb][:], allow_sb[kb][:], FUNC.Copy, bias=-SHUT, scale=SHUT)
+            nc.gpsimd.tensor_scalar(shut[kb][:], allow_sb[kb][:], SHUT, -SHUT, MULT, ADD)
 
         with (
             tc.tile_pool(name="late", bufs=1) as late,
-            tc.tile_pool(name="soft", bufs=2) as soft,
-            tc.tile_pool(name="tiny", bufs=4) as tiny,
-            tc.tile_pool(name="tail", bufs=3) as tail,
-            tc.tile_pool(name="store", bufs=4) as store,
+            tc.tile_pool(name="tiny", bufs=6) as tiny,
+            tc.tile_pool(name="tail", bufs=2) as tail,
+            tc.tile_pool(name="store", bufs=2 * CB) as store,
         ):
             weights = late.tile([P, NB, N], BF16, name="weights")
-            score_ps, a = {}, {}
+            hc = [late.tile([P, N], F32, name=f"hc{m}") for m in range(CB)]
+            var = late.tile([P, N], F32, name="var")
+            score_ps, a, zc, sq_bf = {}, {}, {}, {}
+
+            def centre_h(half):
+                span = slice(half * HALF, (half + 1) * HALF)
+                mu_ps = psum_acc.tile([P, HALF], F32, tag="acc")
+                for c in range(CB):
+                    nc.tensor.matmul(
+                        mu_ps[:], mean_w[:], h_bf[c][:, span], start=(c == 0), stop=(c == CB - 1)
+                    )
+                for m in range(CB):
+                    nc.vector.scalar_tensor_tensor(
+                        hc[m][:, span], h[m][:, span], b_centred[:, m : m + 1], mu_ps[:], ADD, SUB
+                    )
 
             def scores(b):
                 first = max(0, b - BACK)
                 seen = (b + 1 - first) * P
                 score_ps[b] = psum_score.tile([P, SEEN], F32, tag="score", name="score_ps")
-                for d in range(CB):
+                for c in range(CB):
                     nc.tensor.matmul(
                         score_ps[b][:, :seen],
-                        q_bf[d][:, b * P : (b + 1) * P],
-                        k_bf[d][:, first * P : (b + 1) * P],
-                        start=(d == 0),
+                        g_bf[c][:, b * P : (b + 1) * P],
+                        h_bf[c][:, first * P : (b + 1) * P],
+                        start=(c == 0),
                         stop=False,
                     )
                 for kb in range(first, b + 1):
@@ -232,19 +260,12 @@ def tile_autoregressivemodel_b_kernel(
             def softmax(b):
                 first = max(0, b - BACK)
                 seen = (b + 1 - first) * P
-                top = tiny.tile([P, 1], F32)
-                nc.vector.reduce_max(top[:], score_ps[b][:, :seen], axis=ALONG_FREE)
                 neg_top = tiny.tile([P, 1], F32)
-                nc.vector.tensor_scalar_mul(neg_top[:], top[:], -SCALE)
+                nc.vector.reduce_max(neg_top[:], score_ps[b][:, :seen], axis=ALONG_FREE, negate=True)
                 e = soft.tile([P, SEEN], F32)
                 total = tiny.tile([P, 1], F32)
                 nc.scalar.activation(
-                    e[:, :seen],
-                    score_ps[b][:, :seen],
-                    FUNC.Exp,
-                    bias=neg_top[:],
-                    scale=SCALE,
-                    accum_out=total[:],
+                    e[:, :seen], score_ps[b][:, :seen], FUNC.Exp, bias=neg_top[:], accum_out=total[:]
                 )
                 inv_total = tiny.tile([P, 1], F32)
                 nc.vector.reciprocal(inv_total[:], total[:])
@@ -264,25 +285,11 @@ def tile_autoregressivemodel_b_kernel(
                     a_flip[:, :seen].rearrange("p (k j) -> p k j", j=P),
                 )
 
-            for b in range(AHEAD):
-                scores(b)
-            for b in range(NB):
-                for job in late_qk_jobs[3 * b : 3 * b + 3]:
-                    second_half(job)
-                softmax(b)
-                if b + AHEAD < NB:
-                    scores(b + AHEAD)
-                flip(b)
-            for job in u_jobs:
-                second_half(job)
-
-            z, z_bf, zc, sq_bf = {}, {}, {}, {}
-
             def weighted_sum(c):
                 j0, b0, b1 = c * CHUNK, 2 * c, 2 * c + 1
                 key_blocks = [b0] + [kb for kb in range(max(0, b0 - BACK), b1 + 1) if kb != b0]
-                z[c] = [tail.tile([P, CHUNK], F32, name=f"z{m}") for m in range(CB)]
-                z_bf[c] = [tail.tile([P, CHUNK], BF16, name=f"z_bf{m}") for m in range(CB)]
+                zc[c] = [late.tile([P, CHUNK], F32, name=f"zc{c}{m}") for m in range(CB)]
+                sq_bf[c] = [tail.tile([P, CHUNK], BF16, name=f"sq_bf{m}") for m in range(CB)]
                 for m in range(CB):
                     z_ps = psum_acc.tile([P, CHUNK], F32, tag="acc")
                     for kb in key_blocks:
@@ -295,34 +302,25 @@ def tile_autoregressivemodel_b_kernel(
                             start=(kb == key_blocks[0]),
                             stop=(kb == key_blocks[-1]),
                         )
-                    nc.vector.scalar_tensor_tensor(
-                        z[c][m][:], z_ps[:], bo_col[m], h[m][:, j0 : j0 + CHUNK], ADD, ADD
-                    )
-                    nc.vector.tensor_copy(z_bf[c][m][:], z[c][m][:])
-
-            def centre(c):
-                mu_ps = psum_stat.tile([P, CHUNK], F32, tag="stat")
-                for m in range(CB):
-                    nc.tensor.matmul(
-                        mu_ps[:], mean_w[:], z_bf[c][m][:], start=(m == 0), stop=(m == CB - 1)
-                    )
-                zc[c] = [tail.tile([P, CHUNK], F32, name=f"zc{m}") for m in range(CB)]
-                sq_bf[c] = [tail.tile([P, CHUNK], BF16, name=f"sq_bf{m}") for m in range(CB)]
-                for m in range(CB):
-                    nc.vector.tensor_tensor(zc[c][m][:], z[c][m][:], mu_ps[:], SUB)
+                    nc.vector.tensor_tensor(zc[c][m][:], z_ps[:], hc[m][:, j0 : j0 + CHUNK], ADD)
                     nc.scalar.activation(sq_bf[c][m][:], zc[c][m][:], FUNC.Square)
 
-            def normalise(c):
-                j0 = c * CHUNK
+            def variance(c):
                 var_ps = psum_stat.tile([P, CHUNK], F32, tag="stat")
                 for m in range(CB):
                     nc.tensor.matmul(
                         var_ps[:], mean_w[:], sq_bf[c][m][:], start=(m == 0), stop=(m == CB - 1)
                     )
-                rstd = tail.tile([P, CHUNK], F32)
-                nc.scalar.activation(rstd[:], var_ps[:], FUNC.Abs_reciprocal_sqrt, bias=eps_col[:])
+                nc.scalar.copy(var[:, c * CHUNK : (c + 1) * CHUNK], var_ps[:])
+
+            def normalise(c):
+                j0 = c * CHUNK
+                rstd = finish.tile([P, CHUNK], F32)
+                nc.scalar.activation(
+                    rstd[:], var[:, j0 : j0 + CHUNK], FUNC.Abs_reciprocal_sqrt, bias=eps_col[:]
+                )
                 for m in range(CB):
-                    normed = tail.tile([P, CHUNK], F32)
+                    normed = finish.tile([P, CHUNK], F32)
                     nc.vector.tensor_tensor(normed[:], zc[c][m][:], rstd[:], MULT)
                     o = store.tile([P, CHUNK], F32)
                     nc.scalar.activation(
@@ -330,10 +328,30 @@ def tile_autoregressivemodel_b_kernel(
                     )
                     nc.sync.dma_start(out[m * P : (m + 1) * P, j0 : j0 + CHUNK], o[:])
 
-            for c in range(NCHUNK + 2):
-                if c < NCHUNK:
-                    weighted_sum(c)
-                if 0 <= c - 1 < NCHUNK:
-                    centre(c - 1)
-                if c - 2 >= 0:
-                    normalise(c - 2)
+            with tc.tile_pool(name="soft", bufs=3) as soft:
+                for job in g_jobs[:CB]:
+                    second_half(job)
+                for b in range(AHEAD):
+                    scores(b)
+                late_g_jobs = g_jobs[CB:]
+                for step in range(NB):
+                    softmax(step)
+                    for job in late_g_jobs[2 * step : 2 * step + 2]:
+                        second_half(job)
+                    if step + AHEAD < NB:
+                        scores(step + AHEAD)
+                    flip(step)
+                    second_half(u_jobs[step])
+                    if step in (0, 3):
+                        centre_h(step // 3)
+                    if step >= 2 and step % 2 == 0:
+                        weighted_sum((step - 2) // 2)
+                    if step >= 3 and step % 2 == 1:
+                        variance((step - 3) // 2)
+
+            with tc.tile_pool(name="finish", bufs=4) as finish:
+                weighted_sum(NCHUNK - 1)
+                for c in range(NCHUNK - 1):
+                    normalise(c)
+                variance(NCHUNK - 1)
+                normalise(NCHUNK - 1)

@@ -39,10 +39,7 @@ def tile_autoregressivemodel_b_kernel(
     nc = tc.nc
     with (
         tc.tile_pool(name="held", bufs=1) as held,
-        tc.psum_pool(name="psum_acc", bufs=4) as psum_acc,
-        tc.psum_pool(name="psum_score", bufs=AHEAD) as psum_score,
-        tc.psum_pool(name="psum_flip", bufs=1) as psum_flip,
-        tc.psum_pool(name="psum_stat", bufs=1) as psum_stat,
+        tc.psum_pool(name="psum", bufs=8) as psum,
     ):
         offsets = held.tile([P, N // 16], U16, name="offsets")
         nc.sync.dma_start(offsets[:], offs)
@@ -88,7 +85,7 @@ def tile_autoregressivemodel_b_kernel(
             warm = held.tile([P, 1], F32, name="warm")
             nc.scalar.activation(warm[:], eps_col[:], FUNC.Exp)
 
-            cols_ps = psum_flip.tile([P, P], F32, tag="flip")
+            cols_ps = psum.tile([P, P], F32, tag="bank")
             nc.tensor.transpose(cols_ps[:], rows[:], ident_f32[:])
             cols = held.tile([P, 4 * CB], F32, name="cols")
             nc.vector.tensor_copy(cols[:], cols_ps[:, : 4 * CB])
@@ -98,7 +95,7 @@ def tile_autoregressivemodel_b_kernel(
             def flipped(name):
                 w_flip = held.tile([P, CB, D], BF16, name=name + "_flip")
                 for d in range(CB):
-                    flip_ps = psum_acc.tile([P, D], BF16, tag="acc")
+                    flip_ps = psum.tile([P, D], BF16, tag="bank")
                     for c in range(CB):
                         nc.tensor.transpose(
                             flip_ps[:, c * P : (c + 1) * P],
@@ -112,7 +109,7 @@ def tile_autoregressivemodel_b_kernel(
                 return w_flip
 
             def merged(row_block, left_flip, right):
-                product_ps = psum_acc.tile([P, D], F32, tag="acc", name="product_ps")
+                product_ps = psum.tile([P, D], F32, tag="bank", name="product_ps")
                 for d in range(CB):
                     nc.tensor.matmul(
                         product_ps[:],
@@ -143,7 +140,7 @@ def tile_autoregressivemodel_b_kernel(
 
             bv_bf = held.tile([P, CB], BF16, name="bv_bf")
             nc.vector.tensor_copy(bv_bf[:], cols[:, 3 * CB : 4 * CB])
-            bvo_ps = psum_flip.tile([P, CB], F32, tag="flip")
+            bvo_ps = psum.tile([P, CB], F32, tag="bank")
             for m in range(CB):
                 for d in range(CB):
                     nc.tensor.matmul(
@@ -155,7 +152,7 @@ def tile_autoregressivemodel_b_kernel(
                     )
             b_col = held.tile([P, CB], F32, name="b_col")
             nc.vector.tensor_tensor(b_col[:], bvo_ps[:], cols[:, :CB], ADD)
-            b_sum_ps = psum_flip.tile([P, CB], F32, tag="flip")
+            b_sum_ps = psum.tile([P, CB], F32, tag="bank")
             nc.tensor.matmul(b_sum_ps[:], mean_w_f32[:], b_col[:])
             b_mean = held.tile([P, 1], F32, name="b_mean")
             nc.vector.reduce_sum(b_mean[:], b_sum_ps[:], axis=ALONG_FREE)
@@ -179,7 +176,7 @@ def tile_autoregressivemodel_b_kernel(
 
         def project(job, blocks):
             kind, index, half = job
-            acc = psum_acc.tile([P, HALF], F32, tag="acc")
+            acc = psum.tile([P, HALF], F32, tag="bank")
             for c in blocks:
                 if kind == "u":
                     stationary = h_bf[c][:, index * P : (index + 1) * P]
@@ -217,16 +214,17 @@ def tile_autoregressivemodel_b_kernel(
             tc.tile_pool(name="late", bufs=1) as late,
             tc.tile_pool(name="tiny", bufs=6) as tiny,
             tc.tile_pool(name="tail", bufs=2) as tail,
-            tc.tile_pool(name="store", bufs=2 * CB) as store,
+            tc.tile_pool(name="normed", bufs=2 * CB) as normed_pool,
+            tc.tile_pool(name="store", bufs=NCHUNK * CB) as store,
         ):
             weights = late.tile([P, NB, N], BF16, name="weights")
             hc = [late.tile([P, N], F32, name=f"hc{m}") for m in range(CB)]
-            var = late.tile([P, N], F32, name="var")
+            var = late.tile([P, N - CHUNK], F32, name="var")
             score_ps, a, zc, sq_bf = {}, {}, {}, {}
 
             def centre_h(half):
                 span = slice(half * HALF, (half + 1) * HALF)
-                mu_ps = psum_acc.tile([P, HALF], F32, tag="acc")
+                mu_ps = psum.tile([P, HALF], F32, tag="bank")
                 for c in range(CB):
                     nc.tensor.matmul(
                         mu_ps[:], mean_w[:], h_bf[c][:, span], start=(c == 0), stop=(c == CB - 1)
@@ -239,7 +237,7 @@ def tile_autoregressivemodel_b_kernel(
             def scores(b):
                 first = max(0, b - BACK)
                 seen = (b + 1 - first) * P
-                score_ps[b] = psum_score.tile([P, SEEN], F32, tag="score", name="score_ps")
+                score_ps[b] = psum.tile([P, SEEN], F32, tag="bank", name="score_ps")
                 for c in range(CB):
                     nc.tensor.matmul(
                         score_ps[b][:, :seen],
@@ -275,7 +273,7 @@ def tile_autoregressivemodel_b_kernel(
             def flip(b):
                 first = max(0, b - BACK)
                 seen = (b + 1 - first) * P
-                a_flip = psum_flip.tile([P, SEEN], BF16, tag="flip")
+                a_flip = psum.tile([P, SEEN], BF16, tag="bank")
                 for kk in range(b + 1 - first):
                     nc.tensor.transpose(
                         a_flip[:, kk * P : (kk + 1) * P], a[b][:, kk * P : (kk + 1) * P], ident_bf16[:]
@@ -291,7 +289,7 @@ def tile_autoregressivemodel_b_kernel(
                 zc[c] = [late.tile([P, CHUNK], F32, name=f"zc{c}{m}") for m in range(CB)]
                 sq_bf[c] = [tail.tile([P, CHUNK], BF16, name=f"sq_bf{m}") for m in range(CB)]
                 for m in range(CB):
-                    z_ps = psum_acc.tile([P, CHUNK], F32, tag="acc")
+                    z_ps = psum.tile([P, CHUNK], F32, tag="bank")
                     for kb in key_blocks:
                         lo = max(b0, kb) * P
                         hi = (min(b1, kb + BACK) + 1) * P
@@ -306,26 +304,27 @@ def tile_autoregressivemodel_b_kernel(
                     nc.scalar.activation(sq_bf[c][m][:], zc[c][m][:], FUNC.Square)
 
             def variance(c):
-                var_ps = psum_stat.tile([P, CHUNK], F32, tag="stat")
+                var_ps = psum.tile([P, CHUNK], F32, tag="bank")
                 for m in range(CB):
                     nc.tensor.matmul(
                         var_ps[:], mean_w[:], sq_bf[c][m][:], start=(m == 0), stop=(m == CB - 1)
                     )
-                nc.scalar.copy(var[:, c * CHUNK : (c + 1) * CHUNK], var_ps[:])
+                return var_ps
 
-            def normalise(c):
+            def normalise(c, variance_of_c):
                 j0 = c * CHUNK
                 rstd = finish.tile([P, CHUNK], F32)
-                nc.scalar.activation(
-                    rstd[:], var[:, j0 : j0 + CHUNK], FUNC.Abs_reciprocal_sqrt, bias=eps_col[:]
-                )
+                nc.scalar.activation(rstd[:], variance_of_c, FUNC.Abs_reciprocal_sqrt, bias=eps_col[:])
                 for m in range(CB):
-                    normed = finish.tile([P, CHUNK], F32)
+                    normed = normed_pool.tile([P, CHUNK], F32)
                     nc.vector.tensor_tensor(normed[:], zc[c][m][:], rstd[:], MULT)
                     o = store.tile([P, CHUNK], F32)
-                    nc.scalar.activation(
-                        o[:], normed[:], FUNC.Identity, bias=bias_col[m], scale=gain_col[m]
-                    )
+                    if m % 2 == 0:
+                        nc.scalar.activation(
+                            o[:], normed[:], FUNC.Identity, bias=bias_col[m], scale=gain_col[m]
+                        )
+                    else:
+                        nc.gpsimd.tensor_scalar(o[:], normed[:], gain_col[m], bias_col[m], MULT, ADD)
                     nc.sync.dma_start(out[m * P : (m + 1) * P, j0 : j0 + CHUNK], o[:])
 
             with tc.tile_pool(name="soft", bufs=3) as soft:
@@ -347,11 +346,11 @@ def tile_autoregressivemodel_b_kernel(
                     if step >= 2 and step % 2 == 0:
                         weighted_sum((step - 2) // 2)
                     if step >= 3 and step % 2 == 1:
-                        variance((step - 3) // 2)
+                        c = (step - 3) // 2
+                        nc.scalar.copy(var[:, c * CHUNK : (c + 1) * CHUNK], variance(c)[:])
 
             with tc.tile_pool(name="finish", bufs=4) as finish:
                 weighted_sum(NCHUNK - 1)
                 for c in range(NCHUNK - 1):
-                    normalise(c)
-                variance(NCHUNK - 1)
-                normalise(NCHUNK - 1)
+                    normalise(c, var[:, c * CHUNK : (c + 1) * CHUNK])
+                normalise(NCHUNK - 1, variance(NCHUNK - 1)[:])

@@ -317,14 +317,17 @@ def tile_autoregressivemodel_b_kernel(
                 nc.scalar.activation(rstd[:], variance_of_c, FUNC.Abs_reciprocal_sqrt, bias=eps_col[:])
                 for m in range(CB):
                     normed = normed_pool.tile([P, CHUNK], F32)
-                    nc.vector.tensor_tensor(normed[:], zc[c][m][:], rstd[:], MULT)
                     o = store.tile([P, CHUNK], F32)
                     if m % 2 == 0:
+                        nc.vector.tensor_tensor(normed[:], zc[c][m][:], rstd[:], MULT)
                         nc.scalar.activation(
                             o[:], normed[:], FUNC.Identity, bias=bias_col[m], scale=gain_col[m]
                         )
                     else:
-                        nc.gpsimd.tensor_scalar(o[:], normed[:], gain_col[m], bias_col[m], MULT, ADD)
+                        nc.vector.scalar_tensor_tensor(
+                            normed[:], zc[c][m][:], gain_col[m], rstd[:], MULT, MULT
+                        )
+                        nc.vector.tensor_scalar_add(o[:], normed[:], bias_col[m])
                     nc.sync.dma_start(out[m * P : (m + 1) * P, j0 : j0 + CHUNK], o[:])
 
             with tc.tile_pool(name="soft", bufs=3) as soft:

@@ -208,7 +208,7 @@ def tile_autoregressivemodel_b_kernel(
 
         shut = [held.tile([P, served[kb]], BF16, name=f"shut{kb}") for kb in range(NB)]
         for kb in range(NB):
-            nc.gpsimd.tensor_scalar(shut[kb][:], allow_sb[kb][:], SHUT, -SHUT, MULT, ADD)
+            nc.scalar.activation(shut[kb][:], allow_sb[kb][:], FUNC.Copy, bias=-SHUT, scale=SHUT)
 
         with (
             tc.tile_pool(name="late", bufs=1) as late,

@@ -22,11 +22,12 @@ HALF = 512
 REACH = WIN * GRID + WIN
 BACK = -(-REACH // P)
 SEEN = (BACK + 1) * P
+SERVED = -(-(P + REACH) // (P // 2)) * (P // 2)
 CHUNK = 2 * P
 NCHUNK = N // CHUNK
 SCALE = 1.0 / math.sqrt(D)
 SHUT = 1e30
-AHEAD = 2
+AHEAD = 3
 
 NEAR = sum(GRID - d for d in range(1, WIN + 1))
 PAIRS = NEAR * (GRID + 2 * NEAR) + GRID * (GRID + NEAR)
@@ -60,6 +61,7 @@ def tile_autoregressivemodel_b_kernel(
         allow_sb = [held.tile([P, served[kb]], F32, name=f"allow_sb{kb}") for kb in range(NB)]
         h = [held.tile([P, N], F32, name=f"h{c}") for c in range(CB)]
         h_bf = [held.tile([P, N], BF16, name=f"h_bf{c}") for c in range(CB)]
+        h_sum = {c: held.tile([P, N], BF16 if c == CB - 1 else F32, name=f"h_sum{c}") for c in range(1, CB)}
 
         with tc.tile_pool(name="lookup", bufs=1) as lookup:
             table_sb = [lookup.tile([P, WORDS], F32, name=f"table_sb{c}") for c in range(CB)]
@@ -167,6 +169,9 @@ def tile_autoregressivemodel_b_kernel(
                         h[c][:, span], table_sb[c][:].indirect(piece), pos_sb[c][:, span], ADD
                     )
                     nc.vector.tensor_copy(h_bf[c][:, span], h[c][:, span])
+                    if c > 0:
+                        so_far = h[0] if c == 1 else h_sum[c - 1]
+                        nc.gpsimd.tensor_tensor(h_sum[c][:, span], so_far[:, span], h[c][:, span], ADD)
 
         g_bf = [held.tile([P, N], BF16, name=f"g_bf{c}") for c in range(CB)]
         u_bf = [held.tile([P, D], BF16, name=f"u_bf{i}") for i in range(NB)]
@@ -225,10 +230,7 @@ def tile_autoregressivemodel_b_kernel(
             def centre_h(half):
                 span = slice(half * HALF, (half + 1) * HALF)
                 mu_ps = psum.tile([P, HALF], F32, tag="bank")
-                for c in range(CB):
-                    nc.tensor.matmul(
-                        mu_ps[:], mean_w[:], h_bf[c][:, span], start=(c == 0), stop=(c == CB - 1)
-                    )
+                nc.tensor.matmul(mu_ps[:], mean_w[:], h_sum[CB - 1][:, span])
                 for m in range(CB):
                     nc.vector.scalar_tensor_tensor(
                         hc[m][:, span], h[m][:, span], b_centred[:, m : m + 1], mu_ps[:], ADD, SUB
@@ -292,7 +294,7 @@ def tile_autoregressivemodel_b_kernel(
                     z_ps = psum.tile([P, CHUNK], F32, tag="bank")
                     for kb in key_blocks:
                         lo = max(b0, kb) * P
-                        hi = (min(b1, kb + BACK) + 1) * P
+                        hi = min((b1 + 1) * P, kb * P + SERVED)
                         nc.tensor.matmul(
                             z_ps[:, lo - j0 : hi - j0],
                             u_bf[kb][:, m * P : (m + 1) * P],
@@ -330,7 +332,7 @@ def tile_autoregressivemodel_b_kernel(
                         nc.vector.tensor_scalar_add(o[:], normed[:], bias_col[m])
                     nc.sync.dma_start(out[m * P : (m + 1) * P, j0 : j0 + CHUNK], o[:])
 
-            with tc.tile_pool(name="soft", bufs=3) as soft:
+            with tc.tile_pool(name="soft", bufs=4) as soft:
                 for job in g_jobs[:CB]:
                     second_half(job)
                 for b in range(AHEAD):

@@ -19,15 +19,17 @@ EPS = 1e-5
 CB = D // P
 NB = N // P
 HALF = 512
-REACH = WIN * GRID + WIN
+REACH = WIN * GRID
+SEEN = REACH + P
+SERVED = P + REACH
 BACK = -(-REACH // P)
-SEEN = (BACK + 1) * P
-SERVED = -(-(P + REACH) // (P // 2)) * (P // 2)
+PAD = BACK * P - REACH
 CHUNK = 2 * P
 NCHUNK = N // CHUNK
 SCALE = 1.0 / math.sqrt(D)
 SHUT = 1e30
 AHEAD = 3
+ORDER = [*range(1, NB), 0]
 
 NEAR = sum(GRID - d for d in range(1, WIN + 1))
 PAIRS = NEAR * (GRID + 2 * NEAR) + GRID * (GRID + NEAR)
@@ -42,6 +44,11 @@ def tile_autoregressivemodel_b_kernel(
         tc.tile_pool(name="held", bufs=1) as held,
         tc.psum_pool(name="psum", bufs=8) as psum,
     ):
+        weight_sb = {}
+        for name, w in (("wv", wv), ("wo", wo), ("wq", wq), ("wk", wk)):
+            weight_sb[name] = held.tile([P, CB, D], BF16, name=name + "_sb")
+            nc.sync.dma_start(weight_sb[name][:], w.rearrange("(c p) d -> p c d", p=P))
+
         offsets = held.tile([P, N // 16], U16, name="offsets")
         nc.sync.dma_start(offsets[:], offs)
 
@@ -52,13 +59,7 @@ def tile_autoregressivemodel_b_kernel(
                 rows[k * CB : (k + 1) * CB, :], vec.rearrange("(c p) o -> c (p o)", p=P)
             )
 
-        weight_sb = {}
-        for name, w in (("wq", wq), ("wk", wk), ("wv", wv), ("wo", wo)):
-            weight_sb[name] = held.tile([P, CB, D], BF16, name=name + "_sb")
-            nc.sync.dma_start(weight_sb[name][:], w.rearrange("(c p) d -> p c d", p=P))
-
-        served = [min(SEEN, N - kb * P) for kb in range(NB)]
-        allow_sb = [held.tile([P, served[kb]], F32, name=f"allow_sb{kb}") for kb in range(NB)]
+        allow_sb = held.tile([P, (BACK + 1) * P], F32, name="allow_sb")
         h = [held.tile([P, N], F32, name=f"h{c}") for c in range(CB)]
         h_bf = [held.tile([P, N], BF16, name=f"h_bf{c}") for c in range(CB)]
         h_sum = {c: held.tile([P, N], BF16 if c == CB - 1 else F32, name=f"h_sum{c}") for c in range(1, CB)}
@@ -69,10 +70,7 @@ def tile_autoregressivemodel_b_kernel(
             for c in range(CB):
                 nc.sync.dma_start(pos_sb[c][:], pos[c * P : (c + 1) * P, :])
                 nc.sync.dma_start(table_sb[c][:], table[c * P : (c + 1) * P, :])
-            for kb in range(NB):
-                nc.sync.dma_start(
-                    allow_sb[kb][:], allow[kb * P : (kb + 1) * P, kb * P : kb * P + served[kb]]
-                )
+            nc.sync.dma_start(allow_sb[:], allow[:P, : (BACK + 1) * P])
 
             ident_f32 = held.tile([P, P], F32, name="ident_f32")
             make_identity(nc, ident_f32[:])
@@ -80,6 +78,8 @@ def tile_autoregressivemodel_b_kernel(
             nc.vector.tensor_copy(ident_bf16[:], ident_f32[:])
             mean_w = held.tile([P, P], BF16, name="mean_w")
             nc.vector.memset(mean_w[:], 1.0 / D)
+            neg_mean_w = held.tile([P, P], BF16, name="neg_mean_w")
+            nc.vector.memset(neg_mean_w[:], -1.0 / D)
             mean_w_f32 = held.tile([P, P], F32, name="mean_w_f32")
             nc.vector.memset(mean_w_f32[:], 1.0 / D)
             eps_col = held.tile([P, 1], F32, name="eps_col")
@@ -87,19 +87,16 @@ def tile_autoregressivemodel_b_kernel(
             warm = held.tile([P, 1], F32, name="warm")
             nc.scalar.activation(warm[:], eps_col[:], FUNC.Exp)
 
-            cols_ps = psum.tile([P, P], F32, tag="bank")
-            nc.tensor.transpose(cols_ps[:], rows[:], ident_f32[:])
-            cols = held.tile([P, 4 * CB], F32, name="cols")
-            nc.vector.tensor_copy(cols[:], cols_ps[:, : 4 * CB])
-            gain_col = [cols[:, CB + m : CB + m + 1] for m in range(CB)]
-            bias_col = [cols[:, 2 * CB + m : 2 * CB + m + 1] for m in range(CB)]
+            a = [held.tile([P, (min(b, BACK) + 1) * P], BF16, name=f"a{b}") for b in range(NB)]
+            for b in range(BACK, NB):
+                nc.gpsimd.memset(a[b][:, :PAD], 0.0)
 
             def flipped(name):
                 w_flip = held.tile([P, CB, D], BF16, name=name + "_flip")
                 for d in range(CB):
                     flip_ps = psum.tile([P, D], BF16, tag="bank")
                     for c in range(CB):
-                        nc.tensor.transpose(
+                        nc.tensor.matmul(
                             flip_ps[:, c * P : (c + 1) * P],
                             weight_sb[name][:, c, d * P : (d + 1) * P],
                             ident_bf16[:],
@@ -128,17 +125,24 @@ def tile_autoregressivemodel_b_kernel(
                 nc.vector.tensor_scalar_mul(neg_mean[:], neg_mean[:], -1.0 / D)
                 nc.scalar.activation(result, product_ps[:], FUNC.Identity, bias=neg_mean[:])
 
+            wv_flip = flipped("wv")
             wq_flip = flipped("wq")
             wk_flip = flipped("wk")
+            wvo = held.tile([P, CB, D], BF16, name="wvo")
+            for c in range(CB):
+                centred_copy(wvo[:, c, :], merged(c, wv_flip, weight_sb["wo"]), f"wvo{c}")
             wqk = held.tile([P, CB, D], BF16, name="wqk")
             for c2 in range(CB):
                 nc.scalar.activation(
                     wqk[:, c2, :], merged(c2, wq_flip, wk_flip)[:], FUNC.Copy, scale=SCALE
                 )
-            wv_flip = flipped("wv")
-            wvo = held.tile([P, CB, D], BF16, name="wvo")
-            for c in range(CB):
-                centred_copy(wvo[:, c, :], merged(c, wv_flip, weight_sb["wo"]), f"wvo{c}")
+
+            cols_ps = psum.tile([P, P], F32, tag="bank")
+            nc.tensor.transpose(cols_ps[:], rows[:], ident_f32[:])
+            cols = held.tile([P, 4 * CB], F32, name="cols")
+            nc.vector.tensor_copy(cols[:], cols_ps[:, : 4 * CB])
+            gain_col = [cols[:, CB + m : CB + m + 1] for m in range(CB)]
+            bias_col = [cols[:, 2 * CB + m : 2 * CB + m + 1] for m in range(CB)]
 
             bv_bf = held.tile([P, CB], BF16, name="bv_bf")
             nc.vector.tensor_copy(bv_bf[:], cols[:, 3 * CB : 4 * CB])
@@ -154,34 +158,39 @@ def tile_autoregressivemodel_b_kernel(
                     )
             b_col = held.tile([P, CB], F32, name="b_col")
             nc.vector.tensor_tensor(b_col[:], bvo_ps[:], cols[:, :CB], ADD)
-            b_sum_ps = psum.tile([P, CB], F32, tag="bank")
-            nc.tensor.matmul(b_sum_ps[:], mean_w_f32[:], b_col[:])
-            b_mean = held.tile([P, 1], F32, name="b_mean")
-            nc.vector.reduce_sum(b_mean[:], b_sum_ps[:], axis=ALONG_FREE)
-            b_centred = held.tile([P, CB], F32, name="b_centred")
-            nc.vector.tensor_scalar_sub(b_centred[:], b_col[:], b_mean[:])
+
+            def look_up(c, start, end):
+                nc.vector.tensor_tensor(
+                    h[c][:, start:end],
+                    table_sb[c][:].indirect(offsets[:, start // 16 : end // 16]),
+                    pos_sb[c][:, start:end],
+                    ADD,
+                )
+
+            def round_and_sum(c, start, end):
+                nc.vector.tensor_copy(h_bf[c][:, start:end], h[c][:, start:end])
+                if c > 0:
+                    so_far = h[0] if c == 1 else h_sum[c - 1]
+                    nc.gpsimd.tensor_tensor(
+                        h_sum[c][:, start:end], so_far[:, start:end], h[c][:, start:end], ADD
+                    )
 
             for c in range(CB):
-                for half in range(N // HALF):
-                    span = slice(half * HALF, (half + 1) * HALF)
-                    piece = offsets[:, half * HALF // 16 : (half + 1) * HALF // 16]
-                    nc.vector.tensor_tensor(
-                        h[c][:, span], table_sb[c][:].indirect(piece), pos_sb[c][:, span], ADD
-                    )
-                    nc.vector.tensor_copy(h_bf[c][:, span], h[c][:, span])
-                    if c > 0:
-                        so_far = h[0] if c == 1 else h_sum[c - 1]
-                        nc.gpsimd.tensor_tensor(h_sum[c][:, span], so_far[:, span], h[c][:, span], ADD)
+                look_up(c, 0, HALF)
+                look_up(c, HALF, HALF + HALF // 2)
+                round_and_sum(c, 0, HALF)
+                look_up(c, HALF + HALF // 2, N)
+                round_and_sum(c, HALF, N)
 
         g_bf = [held.tile([P, N], BF16, name=f"g_bf{c}") for c in range(CB)]
         u_bf = [held.tile([P, D], BF16, name=f"u_bf{i}") for i in range(NB)]
 
-        g_jobs = [("g", c, half) for half in range(N // HALF) for c in range(CB)]
+        g_jobs = [[("g", c, half) for c in range(CB)] for half in range(N // HALF)]
         u_jobs = [("u", i, 0) for i in range(NB)]
 
         def project(job, blocks):
             kind, index, half = job
-            acc = psum.tile([P, HALF], F32, tag="bank")
+            acc = psum.tile([P, HALF], F32, tag="bank", name="acc")
             for c in blocks:
                 if kind == "u":
                     stationary = h_bf[c][:, index * P : (index + 1) * P]
@@ -194,26 +203,47 @@ def tile_autoregressivemodel_b_kernel(
                 )
             return acc
 
-        parked = {job: held.tile([P, HALF], F32, name="parked_%s%d%d" % job) for job in g_jobs + u_jobs}
+        early = {job: (0, 1) for job in g_jobs[1] + u_jobs[:CB]}
+        early.update({job: (0, 1, 2) for job in u_jobs[CB:]})
+        parked = {job: held.tile([P, HALF], F32, name="parked_%s%d%d" % job) for job in early}
 
-        def first_half(job):
-            nc.scalar.copy(parked[job][:], project(job, (0, 1))[:])
-
-        def second_half(job):
+        def result_of(job):
             kind, index, half = job
-            acc = project(job, (2, 3))
             if kind == "u":
-                result = u_bf[index][:]
+                return u_bf[index][:]
+            return g_bf[index][:, half * HALF : (half + 1) * HALF]
+
+        def copy_out(k, result, acc):
+            if k % 2 == 0:
+                nc.scalar.copy(result, acc[:])
             else:
-                result = g_bf[index][:, half * HALF : (half + 1) * HALF]
-            nc.vector.tensor_tensor(result, acc[:], parked[job][:], ADD)
+                nc.vector.tensor_copy(result, acc[:])
 
-        for job in g_jobs + u_jobs:
-            first_half(job)
+        def park(k, job):
+            copy_out(k, parked[job][:], project(job, early[job]))
 
-        shut = [held.tile([P, served[kb]], BF16, name=f"shut{kb}") for kb in range(NB)]
-        for kb in range(NB):
-            nc.scalar.activation(shut[kb][:], allow_sb[kb][:], FUNC.Copy, bias=-SHUT, scale=SHUT)
+        def finish_job(job):
+            late = range(len(early[job]), CB)
+            nc.vector.tensor_tensor(result_of(job), project(job, late)[:], parked[job][:], ADD)
+
+        for k, job in enumerate(g_jobs[1] + u_jobs[:CB]):
+            park(k, job)
+
+        b_sum_ps = psum.tile([P, CB], F32, tag="bank")
+        nc.tensor.matmul(b_sum_ps[:], mean_w_f32[:], b_col[:])
+        b_mean = held.tile([P, 1], F32, name="b_mean")
+        nc.vector.reduce_sum(b_mean[:], b_sum_ps[:], axis=ALONG_FREE)
+        b_centred = held.tile([P, CB], F32, name="b_centred")
+        nc.vector.tensor_scalar_sub(b_centred[:], b_col[:], b_mean[:])
+
+        for k, job in enumerate(g_jobs[0]):
+            copy_out(k, result_of(job), project(job, range(CB)))
+
+        for job in u_jobs[CB:]:
+            park(0, job)
+
+        shut = held.tile([P, (BACK + 1) * P], BF16, name="shut")
+        nc.scalar.activation(shut[:], allow_sb[:], FUNC.Copy, bias=-SHUT, scale=SHUT)
 
         with (
             tc.tile_pool(name="late", bufs=1) as late,
@@ -223,43 +253,36 @@ def tile_autoregressivemodel_b_kernel(
             tc.tile_pool(name="store", bufs=NCHUNK * CB) as store,
         ):
             weights = late.tile([P, NB, N], BF16, name="weights")
-            hc = [late.tile([P, N], F32, name=f"hc{m}") for m in range(CB)]
-            var = late.tile([P, N - CHUNK], F32, name="var")
-            score_ps, a, zc, sq_bf = {}, {}, {}, {}
+            var = {c: late.tile([P, CHUNK], F32, name=f"var{c}") for c in (1, 2)}
+            score_ps, zc, sq_bf = {}, {}, {}
 
-            def centre_h(half):
-                span = slice(half * HALF, (half + 1) * HALF)
-                mu_ps = psum.tile([P, HALF], F32, tag="bank")
-                nc.tensor.matmul(mu_ps[:], mean_w[:], h_sum[CB - 1][:, span])
-                for m in range(CB):
-                    nc.vector.scalar_tensor_tensor(
-                        hc[m][:, span], h[m][:, span], b_centred[:, m : m + 1], mu_ps[:], ADD, SUB
-                    )
+            def met(b):
+                first_key = max(0, b * P - REACH)
+                return first_key, (b + 1) * P - first_key
 
             def scores(b):
-                first = max(0, b - BACK)
-                seen = (b + 1 - first) * P
+                first_key, seen = met(b)
                 score_ps[b] = psum.tile([P, SEEN], F32, tag="bank", name="score_ps")
                 for c in range(CB):
                     nc.tensor.matmul(
                         score_ps[b][:, :seen],
                         g_bf[c][:, b * P : (b + 1) * P],
-                        h_bf[c][:, first * P : (b + 1) * P],
+                        h_bf[c][:, first_key : (b + 1) * P],
                         start=(c == 0),
                         stop=False,
                     )
-                for kb in range(first, b + 1):
+                for kb in range(first_key // P, b + 1):
+                    lo = max(first_key, kb * P)
                     nc.tensor.matmul(
-                        score_ps[b][:, (kb - first) * P : (kb - first + 1) * P],
-                        shut[kb][:, (b - kb) * P : (b - kb + 1) * P],
-                        ident_bf16[:],
+                        score_ps[b][:, lo - first_key : (kb + 1) * P - first_key],
+                        shut[:, (b - kb) * P : (b - kb + 1) * P],
+                        ident_bf16[:, lo - kb * P :],
                         start=False,
                         stop=(kb == b),
                     )
 
             def softmax(b):
-                first = max(0, b - BACK)
-                seen = (b + 1 - first) * P
+                seen = met(b)[1]
                 neg_top = tiny.tile([P, 1], F32)
                 nc.vector.reduce_max(neg_top[:], score_ps[b][:, :seen], axis=ALONG_FREE, negate=True)
                 e = soft.tile([P, SEEN], F32)
@@ -269,29 +292,34 @@ def tile_autoregressivemodel_b_kernel(
                 )
                 inv_total = tiny.tile([P, 1], F32)
                 nc.vector.reciprocal(inv_total[:], total[:])
-                a[b] = soft.tile([P, SEEN], BF16, name="a")
-                nc.scalar.activation(a[b][:, :seen], e[:, :seen], FUNC.Identity, scale=inv_total[:])
+                whole = (min(b, BACK) + 1) * P
+                nc.scalar.activation(
+                    a[b][:, whole - seen :], e[:, :seen], FUNC.Identity, scale=inv_total[:]
+                )
 
             def flip(b):
                 first = max(0, b - BACK)
-                seen = (b + 1 - first) * P
-                a_flip = psum.tile([P, SEEN], BF16, tag="bank")
+                whole = (b + 1 - first) * P
+                a_flip = psum.tile([P, (BACK + 1) * P], BF16, tag="bank")
                 for kk in range(b + 1 - first):
                     nc.tensor.transpose(
                         a_flip[:, kk * P : (kk + 1) * P], a[b][:, kk * P : (kk + 1) * P], ident_bf16[:]
                     )
                 nc.scalar.copy(
                     weights[:, first : b + 1, b * P : (b + 1) * P],
-                    a_flip[:, :seen].rearrange("p (k j) -> p k j", j=P),
+                    a_flip[:, :whole].rearrange("p (k j) -> p k j", j=P),
                 )
 
             def weighted_sum(c):
                 j0, b0, b1 = c * CHUNK, 2 * c, 2 * c + 1
-                key_blocks = [b0] + [kb for kb in range(max(0, b0 - BACK), b1 + 1) if kb != b0]
+                key_blocks = range(max(0, b0 - BACK), b1 + 1)
                 zc[c] = [late.tile([P, CHUNK], F32, name=f"zc{c}{m}") for m in range(CB)]
                 sq_bf[c] = [tail.tile([P, CHUNK], BF16, name=f"sq_bf{m}") for m in range(CB)]
                 for m in range(CB):
                     z_ps = psum.tile([P, CHUNK], F32, tag="bank")
+                    nc.tensor.matmul(
+                        z_ps[:], neg_mean_w[:], h_sum[CB - 1][:, j0 : j0 + CHUNK], start=True, stop=False
+                    )
                     for kb in key_blocks:
                         lo = max(b0, kb) * P
                         hi = min((b1 + 1) * P, kb * P + SERVED)
@@ -299,10 +327,12 @@ def tile_autoregressivemodel_b_kernel(
                             z_ps[:, lo - j0 : hi - j0],
                             u_bf[kb][:, m * P : (m + 1) * P],
                             weights[:, kb, lo:hi],
-                            start=(kb == key_blocks[0]),
+                            start=False,
                             stop=(kb == key_blocks[-1]),
                         )
-                    nc.vector.tensor_tensor(zc[c][m][:], z_ps[:], hc[m][:, j0 : j0 + CHUNK], ADD)
+                    nc.vector.scalar_tensor_tensor(
+                        zc[c][m][:], z_ps[:], b_centred[:, m : m + 1], h[m][:, j0 : j0 + CHUNK], ADD, ADD
+                    )
                     nc.scalar.activation(sq_bf[c][m][:], zc[c][m][:], FUNC.Square)
 
             def variance(c):
@@ -333,29 +363,26 @@ def tile_autoregressivemodel_b_kernel(
                     nc.sync.dma_start(out[m * P : (m + 1) * P, j0 : j0 + CHUNK], o[:])
 
             with tc.tile_pool(name="soft", bufs=4) as soft:
-                for job in g_jobs[:CB]:
-                    second_half(job)
-                for b in range(AHEAD):
+                for b in ORDER[:AHEAD]:
                     scores(b)
-                late_g_jobs = g_jobs[CB:]
-                for step in range(NB):
-                    softmax(step)
-                    for job in late_g_jobs[2 * step : 2 * step + 2]:
-                        second_half(job)
+                for step, b in enumerate(ORDER):
+                    softmax(b)
+                    if step == 0:
+                        for job in g_jobs[1]:
+                            finish_job(job)
                     if step + AHEAD < NB:
-                        scores(step + AHEAD)
-                    flip(step)
-                    second_half(u_jobs[step])
-                    if step in (0, 3):
-                        centre_h(step // 3)
-                    if step >= 2 and step % 2 == 0:
-                        weighted_sum((step - 2) // 2)
+                        scores(ORDER[step + AHEAD])
+                    flip(b)
+                    finish_job(u_jobs[step])
                     if step >= 3 and step % 2 == 1:
-                        c = (step - 3) // 2
-                        nc.scalar.copy(var[:, c * CHUNK : (c + 1) * CHUNK], variance(c)[:])
+                        weighted_sum((step - 1) // 2)
+                    if step >= 4 and step % 2 == 0:
+                        c = (step - 2) // 2
+                        nc.scalar.copy(var[c][:], variance(c)[:])
 
             with tc.tile_pool(name="finish", bufs=4) as finish:
-                weighted_sum(NCHUNK - 1)
-                for c in range(NCHUNK - 1):
-                    normalise(c, var[:, c * CHUNK : (c + 1) * CHUNK])
-                normalise(NCHUNK - 1, variance(NCHUNK - 1)[:])
+                weighted_sum(0)
+                for c in (1, 2):
+                    normalise(c, var[c][:])
+                for c in (3, 0):
+                    normalise(c, variance(c)[:])

@@ -29,6 +29,7 @@ NCHUNK = N // CHUNK
 SCALE = 1.0 / math.sqrt(D)
 SHUT = 1e30
 AHEAD = 3
+U_AHEAD = 2
 ORDER = [*range(1, NB), 0]
 
 NEAR = sum(GRID - d for d in range(1, WIN + 1))
@@ -128,15 +129,6 @@ def tile_autoregressivemodel_b_kernel(
             wv_flip = flipped("wv")
             wq_flip = flipped("wq")
             wk_flip = flipped("wk")
-            wvo = held.tile([P, CB, D], BF16, name="wvo")
-            for c in range(CB):
-                centred_copy(wvo[:, c, :], merged(c, wv_flip, weight_sb["wo"]), f"wvo{c}")
-            wqk = held.tile([P, CB, D], BF16, name="wqk")
-            for c2 in range(CB):
-                nc.scalar.activation(
-                    wqk[:, c2, :], merged(c2, wq_flip, wk_flip)[:], FUNC.Copy, scale=SCALE
-                )
-
             cols_ps = psum.tile([P, P], F32, tag="bank")
             nc.tensor.transpose(cols_ps[:], rows[:], ident_f32[:])
             cols = held.tile([P, 4 * CB], F32, name="cols")
@@ -146,6 +138,10 @@ def tile_autoregressivemodel_b_kernel(
 
             bv_bf = held.tile([P, CB], BF16, name="bv_bf")
             nc.vector.tensor_copy(bv_bf[:], cols[:, 3 * CB : 4 * CB])
+            wvo = held.tile([P, CB, D], BF16, name="wvo")
+            for c in range(CB):
+                centred_copy(wvo[:, c, :], merged(c, wv_flip, weight_sb["wo"]), f"wvo{c}")
+
             bvo_ps = psum.tile([P, CB], F32, tag="bank")
             for m in range(CB):
                 for d in range(CB):
@@ -158,6 +154,19 @@ def tile_autoregressivemodel_b_kernel(
                     )
             b_col = held.tile([P, CB], F32, name="b_col")
             nc.vector.tensor_tensor(b_col[:], bvo_ps[:], cols[:, :CB], ADD)
+
+            wqk = held.tile([P, CB, D], BF16, name="wqk")
+            for c2 in range(CB):
+                nc.scalar.activation(
+                    wqk[:, c2, :], merged(c2, wq_flip, wk_flip)[:], FUNC.Copy, scale=SCALE
+                )
+
+            b_sum_ps = psum.tile([P, CB], F32, tag="bank")
+            nc.tensor.matmul(b_sum_ps[:], mean_w_f32[:], b_col[:])
+            b_mean = held.tile([P, 1], F32, name="b_mean")
+            nc.vector.reduce_sum(b_mean[:], b_sum_ps[:], axis=ALONG_FREE)
+            b_centred = held.tile([P, CB], F32, name="b_centred")
+            nc.vector.tensor_scalar_sub(b_centred[:], b_col[:], b_mean[:])
 
             def look_up(c, start, end):
                 nc.vector.tensor_tensor(
@@ -228,13 +237,6 @@ def tile_autoregressivemodel_b_kernel(
 
         for k, job in enumerate(g_jobs[1] + u_jobs[:CB]):
             park(k, job)
-
-        b_sum_ps = psum.tile([P, CB], F32, tag="bank")
-        nc.tensor.matmul(b_sum_ps[:], mean_w_f32[:], b_col[:])
-        b_mean = held.tile([P, 1], F32, name="b_mean")
-        nc.vector.reduce_sum(b_mean[:], b_sum_ps[:], axis=ALONG_FREE)
-        b_centred = held.tile([P, CB], F32, name="b_centred")
-        nc.vector.tensor_scalar_sub(b_centred[:], b_col[:], b_mean[:])
 
         for k, job in enumerate(g_jobs[0]):
             copy_out(k, result_of(job), project(job, range(CB)))
@@ -363,6 +365,8 @@ def tile_autoregressivemodel_b_kernel(
                     nc.sync.dma_start(out[m * P : (m + 1) * P, j0 : j0 + CHUNK], o[:])
 
             with tc.tile_pool(name="soft", bufs=4) as soft:
+                for job in u_jobs[:U_AHEAD]:
+                    finish_job(job)
                 for b in ORDER[:AHEAD]:
                     scores(b)
                 for step, b in enumerate(ORDER):
@@ -373,7 +377,8 @@ def tile_autoregressivemodel_b_kernel(
                     if step + AHEAD < NB:
                         scores(ORDER[step + AHEAD])
                     flip(b)
-                    finish_job(u_jobs[step])
+                    if step + U_AHEAD < NB:
+                        finish_job(u_jobs[step + U_AHEAD])
                     if step >= 3 and step % 2 == 1:
                         weighted_sum((step - 1) // 2)
                     if step >= 4 and step % 2 == 0:

@@ -176,20 +176,18 @@ def tile_autoregressivemodel_b_kernel(
                     ADD,
                 )
 
-            def round_and_sum(c, start, end):
+            def rounded(c, start, end):
                 nc.vector.tensor_copy(h_bf[c][:, start:end], h[c][:, start:end])
-                if c > 0:
-                    so_far = h[0] if c == 1 else h_sum[c - 1]
-                    nc.gpsimd.tensor_tensor(
-                        h_sum[c][:, start:end], so_far[:, start:end], h[c][:, start:end], ADD
-                    )
 
             for c in range(CB):
                 look_up(c, 0, HALF)
                 look_up(c, HALF, HALF + HALF // 2)
-                round_and_sum(c, 0, HALF)
+                rounded(c, 0, HALF)
                 look_up(c, HALF + HALF // 2, N)
-                round_and_sum(c, HALF, N)
+                rounded(c, HALF, N)
+                if c > 0:
+                    so_far = h[0] if c == 1 else h_sum[c - 1]
+                    nc.gpsimd.tensor_tensor(h_sum[c][:], so_far[:], h[c][:], ADD)
 
         g_bf = [held.tile([P, N], BF16, name=f"g_bf{c}") for c in range(CB)]
         u_bf = [held.tile([P, D], BF16, name=f"u_bf{i}") for i in range(NB)]

@@ -48,14 +48,17 @@ def tile_autoregressivemodel_b_kernel(
         weight_sb = {}
         for name, w in (("wv", wv), ("wo", wo), ("wq", wq), ("wk", wk)):
             weight_sb[name] = held.tile([P, CB, D], BF16, name=name + "_sb")
-            nc.sync.dma_start(weight_sb[name][:], w.rearrange("(c p) d -> p c d", p=P))
+            nc.sync.dma_start(weight_sb[name][:], w.rearrange("(p c) d -> p c d", c=CB))
 
         offsets = held.tile([P, N // 16], U16, name="offsets")
         nc.sync.dma_start(offsets[:], offs)
 
+        bv_sb = held.tile([P, CB], F32, name="bv_sb")
+        nc.sync.dma_start(bv_sb[:], bv.rearrange("(p c) o -> p (c o)", c=CB))
+
         rows = held.tile([P, P], F32, name="rows")
         nc.vector.memset(rows[:], 0.0)
-        for k, vec in enumerate((bo, ln_gain, ln_bias, bv)):
+        for k, vec in enumerate((bo, ln_gain, ln_bias)):
             nc.sync.dma_start(
                 rows[k * CB : (k + 1) * CB, :], vec.rearrange("(c p) o -> c (p o)", p=P)
             )
@@ -99,13 +102,15 @@ def tile_autoregressivemodel_b_kernel(
                     for c in range(CB):
                         nc.tensor.matmul(
                             flip_ps[:, c * P : (c + 1) * P],
-                            weight_sb[name][:, c, d * P : (d + 1) * P],
+                            weight_sb[name][:, c, d::CB],
                             ident_bf16[:],
                         )
+                    in_order = flip_ps[:].rearrange("k (c p) -> k p c", p=P)
+                    result = w_flip[:, d, :].rearrange("k (p c) -> k p c", c=CB)
                     if d % 2 == 0:
-                        nc.scalar.copy(w_flip[:, d, :], flip_ps[:])
+                        nc.scalar.copy(result, in_order)
                     else:
-                        nc.vector.tensor_copy(w_flip[:, d, :], flip_ps[:])
+                        nc.vector.tensor_copy(result, in_order)
                 return w_flip
 
             def merged(row_block, left_flip, right):
@@ -131,13 +136,13 @@ def tile_autoregressivemodel_b_kernel(
             wk_flip = flipped("wk")
             cols_ps = psum.tile([P, P], F32, tag="bank")
             nc.tensor.transpose(cols_ps[:], rows[:], ident_f32[:])
-            cols = held.tile([P, 4 * CB], F32, name="cols")
-            nc.vector.tensor_copy(cols[:], cols_ps[:, : 4 * CB])
+            cols = held.tile([P, 3 * CB], F32, name="cols")
+            nc.vector.tensor_copy(cols[:], cols_ps[:, : 3 * CB])
             gain_col = [cols[:, CB + m : CB + m + 1] for m in range(CB)]
             bias_col = [cols[:, 2 * CB + m : 2 * CB + m + 1] for m in range(CB)]
 
             bv_bf = held.tile([P, CB], BF16, name="bv_bf")
-            nc.vector.tensor_copy(bv_bf[:], cols[:, 3 * CB : 4 * CB])
+            nc.vector.tensor_copy(bv_bf[:], bv_sb[:])
             wvo = held.tile([P, CB, D], BF16, name="wvo")
             for c in range(CB):
                 centred_copy(wvo[:, c, :], merged(c, wv_flip, weight_sb["wo"]), f"wvo{c}")

@@ -142,7 +142,7 @@ def tile_autoregressivemodel_b_kernel(
             bias_col = [cols[:, 2 * CB + m : 2 * CB + m + 1] for m in range(CB)]
 
             bv_bf = held.tile([P, CB], BF16, name="bv_bf")
-            nc.vector.tensor_copy(bv_bf[:], bv_sb[:])
+            nc.gpsimd.tensor_copy(bv_bf[:], bv_sb[:])
             wvo = held.tile([P, CB, D], BF16, name="wvo")
             for c in range(CB):
                 centred_copy(wvo[:, c, :], merged(c, wv_flip, weight_sb["wo"]), f"wvo{c}")

@@ -201,8 +201,12 @@ def tile_autoregressivemodel_b_kernel(
         u_jobs = [("u", i, 0) for i in range(NB)]
 
         def project(job, blocks):
-            kind, index, half = job
             acc = psum.tile([P, HALF], F32, tag="bank", name="acc")
+            add_blocks(job, acc, blocks, blocks)
+            return acc
+
+        def add_blocks(job, acc, blocks, all_blocks):
+            kind, index, half = job
             for c in blocks:
                 if kind == "u":
                     stationary = h_bf[c][:, index * P : (index + 1) * P]
@@ -211,9 +215,8 @@ def tile_autoregressivemodel_b_kernel(
                     stationary = wqk[:, c, index * P : (index + 1) * P]
                     moving = h_bf[c][:, half * HALF : (half + 1) * HALF]
                 nc.tensor.matmul(
-                    acc[:], stationary, moving, start=(c == blocks[0]), stop=(c == blocks[-1])
+                    acc[:], stationary, moving, start=(c == all_blocks[0]), stop=(c == all_blocks[-1])
                 )
-            return acc
 
         early = {job: (0, 1) for job in g_jobs[1] + u_jobs[:CB]}
         early.update({job: (0, 1, 2) for job in u_jobs[CB:]})
@@ -234,9 +237,20 @@ def tile_autoregressivemodel_b_kernel(
         def park(k, job):
             copy_out(k, parked[job][:], project(job, early[job]))
 
+        late_sum = {}
+
+        def open_late(job):
+            late = range(len(early[job]), CB)
+            late_sum[job] = psum.tile([P, HALF], F32, tag="bank", name="late_sum")
+            add_blocks(job, late_sum[job], late[:-1], late)
+
         def finish_job(job):
             late = range(len(early[job]), CB)
-            nc.vector.tensor_tensor(result_of(job), project(job, late)[:], parked[job][:], ADD)
+            if job not in late_sum:
+                late_sum[job] = project(job, late)
+            else:
+                add_blocks(job, late_sum[job], late[-1:], late)
+            nc.vector.tensor_tensor(result_of(job), late_sum[job][:], parked[job][:], ADD)
 
         for k, job in enumerate(g_jobs[1] + u_jobs[:CB]):
             park(k, job)
@@ -246,6 +260,9 @@ def tile_autoregressivemodel_b_kernel(
 
         for job in u_jobs[CB:]:
             park(0, job)
+
+        for job in g_jobs[1]:
+            open_late(job)
 
         shut = held.tile([P, (BACK + 1) * P], BF16, name="shut")
         nc.scalar.activation(shut[:], allow_sb[:], FUNC.Copy, bias=-SHUT, scale=SHUT)
@@ -298,8 +315,8 @@ def tile_autoregressivemodel_b_kernel(
                 inv_total = tiny.tile([P, 1], F32)
                 nc.vector.reciprocal(inv_total[:], total[:])
                 whole = (min(b, BACK) + 1) * P
-                nc.scalar.activation(
-                    a[b][:, whole - seen :], e[:, :seen], FUNC.Identity, scale=inv_total[:]
+                nc.gpsimd.tensor_scalar(
+                    a[b][:, whole - seen :], e[:, :seen], inv_total[:], 1.0, MULT, MULT
                 )
 
             def flip(b):

@@ -24,13 +24,13 @@ SEEN = REACH + P
 SERVED = P + REACH
 BACK = -(-REACH // P)
 PAD = BACK * P - REACH
-CHUNK = 2 * P
-NCHUNK = N // CHUNK
 SCALE = 1.0 / math.sqrt(D)
 SHUT = 1e30
 AHEAD = 3
 U_AHEAD = 2
 ORDER = [*range(1, NB), 0]
+CHUNKS = [(1, 4), (4, 6), (6, 8), (0, 1)]
+WIDEST = 3 * P
 
 NEAR = sum(GRID - d for d in range(1, WIN + 1))
 PAIRS = NEAR * (GRID + 2 * NEAR) + GRID * (GRID + NEAR)
@@ -272,10 +272,10 @@ def tile_autoregressivemodel_b_kernel(
             tc.tile_pool(name="tiny", bufs=6) as tiny,
             tc.tile_pool(name="tail", bufs=2) as tail,
             tc.tile_pool(name="normed", bufs=2 * CB) as normed_pool,
-            tc.tile_pool(name="store", bufs=NCHUNK * CB) as store,
+            tc.tile_pool(name="store", bufs=1) as store,
         ):
             weights = late.tile([P, NB, N], BF16, name="weights")
-            var = {c: late.tile([P, CHUNK], F32, name=f"var{c}") for c in (1, 2)}
+            var = [late.tile([P, WIDEST], F32, name=f"var{c}") for c in range(2)]
             score_ps, zc, sq_bf = {}, {}, {}
 
             def met(b):
@@ -333,18 +333,19 @@ def tile_autoregressivemodel_b_kernel(
                 )
 
             def weighted_sum(c):
-                j0, b0, b1 = c * CHUNK, 2 * c, 2 * c + 1
-                key_blocks = range(max(0, b0 - BACK), b1 + 1)
-                zc[c] = [late.tile([P, CHUNK], F32, name=f"zc{c}{m}") for m in range(CB)]
-                sq_bf[c] = [tail.tile([P, CHUNK], BF16, name=f"sq_bf{m}") for m in range(CB)]
+                b0, b1 = CHUNKS[c]
+                j0, j1 = b0 * P, b1 * P
+                key_blocks = range(max(0, b0 - BACK), b1)
+                zc[c] = [late.tile([P, j1 - j0], F32, name=f"zc{c}{m}") for m in range(CB)]
+                sq_bf[c] = [tail.tile([P, WIDEST], BF16, name=f"sq_bf{m}") for m in range(CB)]
                 for m in range(CB):
-                    z_ps = psum.tile([P, CHUNK], F32, tag="bank")
+                    z_ps = psum.tile([P, j1 - j0], F32, tag="bank")
                     nc.tensor.matmul(
-                        z_ps[:], neg_mean_w[:], h_sum[CB - 1][:, j0 : j0 + CHUNK], start=True, stop=False
+                        z_ps[:], neg_mean_w[:], h_sum[CB - 1][:, j0:j1], start=True, stop=False
                     )
                     for kb in key_blocks:
-                        lo = max(b0, kb) * P
-                        hi = min((b1 + 1) * P, kb * P + SERVED)
+                        lo = max(j0, kb * P)
+                        hi = min(j1, kb * P + SERVED)
                         nc.tensor.matmul(
                             z_ps[:, lo - j0 : hi - j0],
                             u_bf[kb][:, m * P : (m + 1) * P],
@@ -353,36 +354,42 @@ def tile_autoregressivemodel_b_kernel(
                             stop=(kb == key_blocks[-1]),
                         )
                     nc.vector.scalar_tensor_tensor(
-                        zc[c][m][:], z_ps[:], b_centred[:, m : m + 1], h[m][:, j0 : j0 + CHUNK], ADD, ADD
+                        zc[c][m][:], z_ps[:], b_centred[:, m : m + 1], h[m][:, j0:j1], ADD, ADD
                     )
-                    nc.scalar.activation(sq_bf[c][m][:], zc[c][m][:], FUNC.Square)
+                    nc.scalar.activation(sq_bf[c][m][:, : j1 - j0], zc[c][m][:], FUNC.Square)
 
             def variance(c):
-                var_ps = psum.tile([P, CHUNK], F32, tag="bank")
+                width = (CHUNKS[c][1] - CHUNKS[c][0]) * P
+                var_ps = psum.tile([P, width], F32, tag="bank")
                 for m in range(CB):
                     nc.tensor.matmul(
-                        var_ps[:], mean_w[:], sq_bf[c][m][:], start=(m == 0), stop=(m == CB - 1)
+                        var_ps[:], mean_w[:], sq_bf[c][m][:, :width], start=(m == 0), stop=(m == CB - 1)
                     )
                 return var_ps
 
+            def var_of(c):
+                return var[c][:, : (CHUNKS[c][1] - CHUNKS[c][0]) * P]
+
             def normalise(c, variance_of_c):
-                j0 = c * CHUNK
-                rstd = finish.tile([P, CHUNK], F32)
-                nc.scalar.activation(rstd[:], variance_of_c, FUNC.Abs_reciprocal_sqrt, bias=eps_col[:])
+                j0, j1 = CHUNKS[c][0] * P, CHUNKS[c][1] * P
+                rstd_tile = finish.tile([P, WIDEST], F32)
+                rstd = rstd_tile[:, : j1 - j0]
+                nc.scalar.activation(rstd, variance_of_c, FUNC.Abs_reciprocal_sqrt, bias=eps_col[:])
                 for m in range(CB):
-                    normed = normed_pool.tile([P, CHUNK], F32)
-                    o = store.tile([P, CHUNK], F32)
+                    normed_tile = normed_pool.tile([P, WIDEST], F32)
+                    normed = normed_tile[:, : j1 - j0]
+                    o = store.tile([P, j1 - j0], F32, name=f"o{c}{m}")
                     if m % 2 == 0:
-                        nc.vector.tensor_tensor(normed[:], zc[c][m][:], rstd[:], MULT)
+                        nc.vector.tensor_tensor(normed, zc[c][m][:], rstd, MULT)
                         nc.scalar.activation(
-                            o[:], normed[:], FUNC.Identity, bias=bias_col[m], scale=gain_col[m]
+                            o[:], normed, FUNC.Identity, bias=bias_col[m], scale=gain_col[m]
                         )
                     else:
                         nc.vector.scalar_tensor_tensor(
-                            normed[:], zc[c][m][:], gain_col[m], rstd[:], MULT, MULT
+                            normed, zc[c][m][:], gain_col[m], rstd, MULT, MULT
                         )
-                        nc.vector.tensor_scalar_add(o[:], normed[:], bias_col[m])
-                    nc.sync.dma_start(out[m * P : (m + 1) * P, j0 : j0 + CHUNK], o[:])
+                        nc.vector.tensor_scalar_add(o[:], normed, bias_col[m])
+                    nc.sync.dma_start(out[m * P : (m + 1) * P, j0:j1], o[:])
 
             with tc.tile_pool(name="soft", bufs=4) as soft:
                 for job in u_jobs[:U_AHEAD]:
@@ -400,14 +407,15 @@ def tile_autoregressivemodel_b_kernel(
                     if step + U_AHEAD < NB:
                         finish_job(u_jobs[step + U_AHEAD])
                     if step >= 3 and step % 2 == 1:
-                        weighted_sum((step - 1) // 2)
+                        weighted_sum((step - 3) // 2)
                     if step >= 4 and step % 2 == 0:
-                        c = (step - 2) // 2
-                        nc.scalar.copy(var[c][:], variance(c)[:])
+                        c = (step - 4) // 2
+                        var_ps = variance(c)
+                        nc.scalar.copy(var_of(c), var_ps[:])
 
             with tc.tile_pool(name="finish", bufs=4) as finish:
-                weighted_sum(0)
-                for c in (1, 2):
-                    normalise(c, var[c][:])
-                for c in (3, 0):
+                weighted_sum(3)
+                for c in (0, 1):
+                    normalise(c, var_of(c))
+                for c in (2, 3):
                     normalise(c, variance(c)[:])

import math

import concourse.mybir as mybir
from concourse.masks import make_identity

F32, BF16, U16 = mybir.dt.float32, mybir.dt.bfloat16, mybir.dt.uint16
ADD, SUB, MULT = mybir.AluOpType.add, mybir.AluOpType.subtract, mybir.AluOpType.mult
FUNC = mybir.ActivationFunctionType
ALONG_FREE = mybir.AxisListType.X

P = 128
D = 512
WORDS = 4096
N = 1024
GRID = 32
WIN = 9
EPS = 1e-5

CB = D // P
NB = N // P
HALF = 512
REACH = WIN * GRID
SEEN = REACH + P
SERVED = P + REACH
BACK = -(-REACH // P)
PAD = BACK * P - REACH
SCALE = 1.0 / math.sqrt(D)
SHUT = 1e30
AHEAD = 3
U_AHEAD = 2
ORDER = [*range(1, NB), 0]
CHUNKS = [(1, 4), (4, 6), (6, 8), (0, 1)]
WIDEST = 3 * P

NEAR = sum(GRID - d for d in range(1, WIN + 1))
PAIRS = NEAR * (GRID + 2 * NEAR) + GRID * (GRID + NEAR)
FLOPS = 4 * 2 * D * D * N + 2 * 2 * D * PAIRS


def tile_autoregressivemodel_b_kernel(
    tc, table, pos, wq, wk, wv, bv, wo, bo, ln_gain, ln_bias, allow, offs, out
):
    nc = tc.nc
    with (
        tc.tile_pool(name="held", bufs=1) as held,
        tc.psum_pool(name="psum", bufs=8) as psum,
    ):
        weight_sb = {}
        for name, w in (("wv", wv), ("wo", wo), ("wq", wq), ("wk", wk)):
            weight_sb[name] = held.tile([P, CB, D], BF16, name=name + "_sb")
            nc.sync.dma_start(weight_sb[name][:], w.rearrange("(p c) d -> p c d", c=CB))

        offsets = held.tile([P, N // 16], U16, name="offsets")
        nc.sync.dma_start(offsets[:], offs)

        bv_sb = held.tile([P, CB], F32, name="bv_sb")
        nc.sync.dma_start(bv_sb[:], bv.rearrange("(p c) o -> p (c o)", c=CB))

        rows = held.tile([P, P], F32, name="rows")
        nc.vector.memset(rows[:], 0.0)
        for k, vec in enumerate((bo, ln_gain, ln_bias)):
            nc.sync.dma_start(
                rows[k * CB : (k + 1) * CB, :], vec.rearrange("(c p) o -> c (p o)", p=P)
            )

        allow_sb = held.tile([P, (BACK + 1) * P], F32, name="allow_sb")
        h = [held.tile([P, N], F32, name=f"h{c}") for c in range(CB)]
        h_bf = [held.tile([P, N], BF16, name=f"h_bf{c}") for c in range(CB)]
        h_sum = {c: held.tile([P, N], BF16 if c == CB - 1 else F32, name=f"h_sum{c}") for c in range(1, CB)}

        with tc.tile_pool(name="lookup", bufs=1) as lookup:
            table_sb = [lookup.tile([P, WORDS], F32, name=f"table_sb{c}") for c in range(CB)]
            pos_sb = [lookup.tile([P, N], F32, name=f"pos_sb{c}") for c in range(CB)]
            for c in range(CB):
                nc.sync.dma_start(pos_sb[c][:], pos[c * P : (c + 1) * P, :])
                nc.sync.dma_start(table_sb[c][:], table[c * P : (c + 1) * P, :])
            nc.sync.dma_start(allow_sb[:], allow[:P, : (BACK + 1) * P])

            ident_f32 = held.tile([P, P], F32, name="ident_f32")
            make_identity(nc, ident_f32[:])
            ident_bf16 = held.tile([P, P], BF16, name="ident_bf16")
            nc.vector.tensor_copy(ident_bf16[:], ident_f32[:])
            mean_w = held.tile([P, P], BF16, name="mean_w")
            nc.vector.memset(mean_w[:], 1.0 / D)
            neg_mean_w = held.tile([P, P], BF16, name="neg_mean_w")
            nc.vector.memset(neg_mean_w[:], -1.0 / D)
            mean_w_f32 = held.tile([P, P], F32, name="mean_w_f32")
            nc.vector.memset(mean_w_f32[:], 1.0 / D)
            eps_col = held.tile([P, 1], F32, name="eps_col")
            nc.vector.memset(eps_col[:], EPS)
            warm = held.tile([P, 1], F32, name="warm")
            nc.scalar.activation(warm[:], eps_col[:], FUNC.Exp)

            a = [held.tile([P, (min(b, BACK) + 1) * P], BF16, name=f"a{b}") for b in range(NB)]
            for b in range(BACK, NB):
                nc.gpsimd.memset(a[b][:, :PAD], 0.0)

            def flipped(name):
                w_flip = held.tile([P, CB, D], BF16, name=name + "_flip")
                for d in range(CB):
                    flip_ps = psum.tile([P, D], BF16, tag="bank")
                    for c in range(CB):
                        nc.tensor.matmul(
                            flip_ps[:, c * P : (c + 1) * P],
                            weight_sb[name][:, c, d::CB],
                            ident_bf16[:],
                        )
                    in_order = flip_ps[:].rearrange("k (c p) -> k p c", p=P)
                    result = w_flip[:, d, :].rearrange("k (p c) -> k p c", c=CB)
                    if d % 2 == 0:
                        nc.scalar.copy(result, in_order)
                    else:
                        nc.vector.tensor_copy(result, in_order)
                return w_flip

            def merged(row_block, left_flip, right):
                product_ps = psum.tile([P, D], F32, tag="bank", name="product_ps")
                for d in range(CB):
                    nc.tensor.matmul(
                        product_ps[:],
                        left_flip[:, d, row_block * P : (row_block + 1) * P],
                        right[:, d, :],
                        start=(d == 0),
                        stop=(d == CB - 1),
                    )
                return product_ps

            def centred_copy(result, product_ps, name):
                neg_mean = held.tile([P, 1], F32, name="neg_mean_" + name)
                nc.vector.reduce_sum(neg_mean[:], product_ps[:], axis=ALONG_FREE)
                nc.vector.tensor_scalar_mul(neg_mean[:], neg_mean[:], -1.0 / D)
                nc.scalar.activation(result, product_ps[:], FUNC.Identity, bias=neg_mean[:])

            wv_flip = flipped("wv")
            wq_flip = flipped("wq")
            wk_flip = flipped("wk")
            cols_ps = psum.tile([P, P], F32, tag="bank")
            nc.tensor.transpose(cols_ps[:], rows[:], ident_f32[:])
            cols = held.tile([P, 3 * CB], F32, name="cols")
            nc.vector.tensor_copy(cols[:], cols_ps[:, : 3 * CB])
            gain_col = [cols[:, CB + m : CB + m + 1] for m in range(CB)]
            bias_col = [cols[:, 2 * CB + m : 2 * CB + m + 1] for m in range(CB)]

            bv_bf = held.tile([P, CB], BF16, name="bv_bf")
            nc.gpsimd.tensor_copy(bv_bf[:], bv_sb[:])
            wvo = held.tile([P, CB, D], BF16, name="wvo")
            for c in range(CB):
                centred_copy(wvo[:, c, :], merged(c, wv_flip, weight_sb["wo"]), f"wvo{c}")

            bvo_ps = psum.tile([P, CB], F32, tag="bank")
            for m in range(CB):
                for d in range(CB):
                    nc.tensor.matmul(
                        bvo_ps[:, m : m + 1],
                        weight_sb["wo"][:, d, m * P : (m + 1) * P],
                        bv_bf[:, d : d + 1],
                        start=(d == 0),
                        stop=(d == CB - 1),
                    )
            b_col = held.tile([P, CB], F32, name="b_col")
            nc.vector.tensor_tensor(b_col[:], bvo_ps[:], cols[:, :CB], ADD)

            wqk = held.tile([P, CB, D], BF16, name="wqk")
            for c2 in range(CB):
                nc.scalar.activation(
                    wqk[:, c2, :], merged(c2, wq_flip, wk_flip)[:], FUNC.Copy, scale=SCALE
                )

            b_sum_ps = psum.tile([P, CB], F32, tag="bank")
            nc.tensor.matmul(b_sum_ps[:], mean_w_f32[:], b_col[:])
            b_mean = held.tile([P, 1], F32, name="b_mean")
            nc.vector.reduce_sum(b_mean[:], b_sum_ps[:], axis=ALONG_FREE)
            b_centred = held.tile([P, CB], F32, name="b_centred")
            nc.vector.tensor_scalar_sub(b_centred[:], b_col[:], b_mean[:])

            def look_up(c, start, end):
                nc.vector.tensor_tensor(
                    h[c][:, start:end],
                    table_sb[c][:].indirect(offsets[:, start // 16 : end // 16]),
                    pos_sb[c][:, start:end],
                    ADD,
                )

            def rounded(c, start, end):
                nc.vector.tensor_copy(h_bf[c][:, start:end], h[c][:, start:end])

            for c in range(CB):
                look_up(c, 0, HALF)
                look_up(c, HALF, HALF + HALF // 2)
                rounded(c, 0, HALF)
                look_up(c, HALF + HALF // 2, N)
                rounded(c, HALF, N)
                if c > 0:
                    so_far = h[0] if c == 1 else h_sum[c - 1]
                    nc.gpsimd.tensor_tensor(h_sum[c][:], so_far[:], h[c][:], ADD)

        g_bf = [held.tile([P, N], BF16, name=f"g_bf{c}") for c in range(CB)]
        u_bf = [held.tile([P, D], BF16, name=f"u_bf{i}") for i in range(NB)]

        g_jobs = [[("g", c, half) for c in range(CB)] for half in range(N // HALF)]
        u_jobs = [("u", i, 0) for i in range(NB)]

        def project(job, blocks):
            acc = psum.tile([P, HALF], F32, tag="bank", name="acc")
            add_blocks(job, acc, blocks, blocks)
            return acc

        def add_blocks(job, acc, blocks, all_blocks):
            kind, index, half = job
            for c in blocks:
                if kind == "u":
                    stationary = h_bf[c][:, index * P : (index + 1) * P]
                    moving = wvo[:, c, :]
                else:
                    stationary = wqk[:, c, index * P : (index + 1) * P]
                    moving = h_bf[c][:, half * HALF : (half + 1) * HALF]
                nc.tensor.matmul(
                    acc[:], stationary, moving, start=(c == all_blocks[0]), stop=(c == all_blocks[-1])
                )

        early = {job: (0, 1) for job in g_jobs[1] + u_jobs[:CB]}
        early.update({job: (0, 1, 2) for job in u_jobs[CB:]})
        parked = {job: held.tile([P, HALF], F32, name="parked_%s%d%d" % job) for job in early}

        def result_of(job):
            kind, index, half = job
            if kind == "u":
                return u_bf[index][:]
            return g_bf[index][:, half * HALF : (half + 1) * HALF]

        def copy_out(k, result, acc):
            if k % 2 == 0:
                nc.scalar.copy(result, acc[:])
            else:
                nc.vector.tensor_copy(result, acc[:])

        def park(k, job):
            copy_out(k, parked[job][:], project(job, early[job]))

        late_sum = {}

        def open_late(job):
            late = range(len(early[job]), CB)
            late_sum[job] = psum.tile([P, HALF], F32, tag="bank", name="late_sum")
            add_blocks(job, late_sum[job], late[:-1], late)

        def finish_job(job):
            late = range(len(early[job]), CB)
            if job not in late_sum:
                late_sum[job] = project(job, late)
            else:
                add_blocks(job, late_sum[job], late[-1:], late)
            nc.vector.tensor_tensor(result_of(job), late_sum[job][:], parked[job][:], ADD)

        for k, job in enumerate(g_jobs[1] + u_jobs[:CB]):
            park(k, job)

        for k, job in enumerate(g_jobs[0]):
            copy_out(k, result_of(job), project(job, range(CB)))

        for job in u_jobs[CB:]:
            park(0, job)

        for job in g_jobs[1]:
            open_late(job)

        shut = held.tile([P, (BACK + 1) * P], BF16, name="shut")
        nc.scalar.activation(shut[:], allow_sb[:], FUNC.Copy, bias=-SHUT, scale=SHUT)

        with (
            tc.tile_pool(name="late", bufs=1) as late,
            tc.tile_pool(name="tiny", bufs=6) as tiny,
            tc.tile_pool(name="tail", bufs=2) as tail,
            tc.tile_pool(name="normed", bufs=2 * CB) as normed_pool,
            tc.tile_pool(name="store", bufs=1) as store,
        ):
            weights = late.tile([P, NB, N], BF16, name="weights")
            var = [late.tile([P, WIDEST], F32, name=f"var{c}") for c in range(2)]
            score_ps, zc, sq_bf = {}, {}, {}

            def met(b):
                first_key = max(0, b * P - REACH)
                return first_key, (b + 1) * P - first_key

            def scores(b):
                first_key, seen = met(b)
                score_ps[b] = psum.tile([P, SEEN], F32, tag="bank", name="score_ps")
                for c in range(CB):
                    nc.tensor.matmul(
                        score_ps[b][:, :seen],
                        g_bf[c][:, b * P : (b + 1) * P],
                        h_bf[c][:, first_key : (b + 1) * P],
                        start=(c == 0),
                        stop=False,
                    )
                for kb in range(first_key // P, b + 1):
                    lo = max(first_key, kb * P)
                    nc.tensor.matmul(
                        score_ps[b][:, lo - first_key : (kb + 1) * P - first_key],
                        shut[:, (b - kb) * P : (b - kb + 1) * P],
                        ident_bf16[:, lo - kb * P :],
                        start=False,
                        stop=(kb == b),
                    )

            def softmax(b):
                seen = met(b)[1]
                neg_top = tiny.tile([P, 1], F32)
                nc.vector.reduce_max(neg_top[:], score_ps[b][:, :seen], axis=ALONG_FREE, negate=True)
                e = soft.tile([P, SEEN], F32)
                total = tiny.tile([P, 1], F32)
                nc.scalar.activation(
                    e[:, :seen], score_ps[b][:, :seen], FUNC.Exp, bias=neg_top[:], accum_out=total[:]
                )
                inv_total = tiny.tile([P, 1], F32)
                nc.vector.reciprocal(inv_total[:], total[:])
                whole = (min(b, BACK) + 1) * P
                nc.gpsimd.tensor_scalar(
                    a[b][:, whole - seen :], e[:, :seen], inv_total[:], 1.0, MULT, MULT
                )

            def flip(b):
                first = max(0, b - BACK)
                whole = (b + 1 - first) * P
                a_flip = psum.tile([P, (BACK + 1) * P], BF16, tag="bank")
                for kk in range(b + 1 - first):
                    nc.tensor.transpose(
                        a_flip[:, kk * P : (kk + 1) * P], a[b][:, kk * P : (kk + 1) * P], ident_bf16[:]
                    )
                nc.scalar.copy(
                    weights[:, first : b + 1, b * P : (b + 1) * P],
                    a_flip[:, :whole].rearrange("p (k j) -> p k j", j=P),
                )

            def weighted_sum(c):
                b0, b1 = CHUNKS[c]
                j0, j1 = b0 * P, b1 * P
                key_blocks = range(max(0, b0 - BACK), b1)
                zc[c] = [late.tile([P, j1 - j0], F32, name=f"zc{c}{m}") for m in range(CB)]
                sq_bf[c] = [tail.tile([P, WIDEST], BF16, name=f"sq_bf{m}") for m in range(CB)]
                for m in range(CB):
                    z_ps = psum.tile([P, j1 - j0], F32, tag="bank")
                    nc.tensor.matmul(
                        z_ps[:], neg_mean_w[:], h_sum[CB - 1][:, j0:j1], start=True, stop=False
                    )
                    for kb in key_blocks:
                        lo = max(j0, kb * P)
                        hi = min(j1, kb * P + SERVED)
                        nc.tensor.matmul(
                            z_ps[:, lo - j0 : hi - j0],
                            u_bf[kb][:, m * P : (m + 1) * P],
                            weights[:, kb, lo:hi],
                            start=False,
                            stop=(kb == key_blocks[-1]),
                        )
                    nc.vector.scalar_tensor_tensor(
                        zc[c][m][:], z_ps[:], b_centred[:, m : m + 1], h[m][:, j0:j1], ADD, ADD
                    )
                    nc.scalar.activation(sq_bf[c][m][:, : j1 - j0], zc[c][m][:], FUNC.Square)

            def variance(c):
                width = (CHUNKS[c][1] - CHUNKS[c][0]) * P
                var_ps = psum.tile([P, width], F32, tag="bank")
                for m in range(CB):
                    nc.tensor.matmul(
                        var_ps[:], mean_w[:], sq_bf[c][m][:, :width], start=(m == 0), stop=(m == CB - 1)
                    )
                return var_ps

            def var_of(c):
                return var[c][:, : (CHUNKS[c][1] - CHUNKS[c][0]) * P]

            def normalise(c, variance_of_c):
                j0, j1 = CHUNKS[c][0] * P, CHUNKS[c][1] * P
                rstd_tile = finish.tile([P, WIDEST], F32)
                rstd = rstd_tile[:, : j1 - j0]
                nc.scalar.activation(rstd, variance_of_c, FUNC.Abs_reciprocal_sqrt, bias=eps_col[:])
                for m in range(CB):
                    normed_tile = normed_pool.tile([P, WIDEST], F32)
                    normed = normed_tile[:, : j1 - j0]
                    o = store.tile([P, j1 - j0], F32, name=f"o{c}{m}")
                    if m % 2 == 0:
                        nc.vector.tensor_tensor(normed, zc[c][m][:], rstd, MULT)
                        nc.scalar.activation(
                            o[:], normed, FUNC.Identity, bias=bias_col[m], scale=gain_col[m]
                        )
                    else:
                        nc.vector.scalar_tensor_tensor(
                            normed, zc[c][m][:], gain_col[m], rstd, MULT, MULT
                        )
                        nc.vector.tensor_scalar_add(o[:], normed, bias_col[m])
                    nc.sync.dma_start(out[m * P : (m + 1) * P, j0:j1], o[:])

            with tc.tile_pool(name="soft", bufs=4) as soft:
                for job in u_jobs[:U_AHEAD]:
                    finish_job(job)
                for b in ORDER[:AHEAD]:
                    scores(b)
                for step, b in enumerate(ORDER):
                    softmax(b)
                    if step == 0:
                        for job in g_jobs[1]:
                            finish_job(job)
                    if step + AHEAD < NB:
                        scores(ORDER[step + AHEAD])
                    flip(b)
                    if step + U_AHEAD < NB:
                        finish_job(u_jobs[step + U_AHEAD])
                    if step >= 3 and step % 2 == 1:
                        weighted_sum((step - 3) // 2)
                    if step >= 4 and step % 2 == 0:
                        c = (step - 4) // 2
                        var_ps = variance(c)
                        nc.scalar.copy(var_of(c), var_ps[:])

            with tc.tile_pool(name="finish", bufs=4) as finish:
                weighted_sum(3)
                for c in (0, 1):
                    normalise(c, var_of(c))
                for c in (2, 3):
                    normalise(c, variance(c)[:])
